import numpy as np
import ml_dtypes


def mxq(x, axis, fmt="e4m3"):
    dtype, down = {"e4m3": (ml_dtypes.float8_e4m3fn, 7), "e5m2": (ml_dtypes.float8_e5m2, 14)}[fmt]
    v = np.moveaxis(np.asarray(x, np.float32).astype(ml_dtypes.bfloat16).astype(np.float64), axis, -1)
    blocks = v.reshape(v.shape[:-1] + (-1, 32))
    amax = np.abs(blocks).max(-1, keepdims=True)
    byte = np.maximum(np.where(amax > 0, np.frexp(amax)[1] - 1 + 127, 0) - down, 1)
    scale = np.exp2(byte - 127.0)
    codes = (blocks / scale).astype(np.float32).astype(dtype).astype(np.float64)
    return np.moveaxis((codes * scale).reshape(v.shape), -1, axis)


WIDE = False


def mx_kscale(k):
    if not WIDE:
        return np.ones(k)
    levels = np.array([10, -10, 5, -5, 0])
    if k % 512:
        return np.exp2(np.random.permutation(np.resize(levels, k // 32))).repeat(32)
    a = np.empty((k // 512, 16))
    for p in range(k // 512):
        a[p, :8] = np.random.permutation(np.resize(levels, 8))
        for g in range(8):
            far = levels[np.abs(levels - a[p, g]) >= 10]
            a[p, g + 8] = far[np.random.randint(len(far))]
    return np.exp2(a.ravel()).repeat(32)


BF16 = ml_dtypes.bfloat16


def bf(x):
    return np.asarray(x, np.float32).astype(BF16)


def f64(x):
    return np.asarray(x).astype(np.float64)


B, S, E, H, KVH, HD = 1, 512, 2048, 16, 4, 128
THETA = 10000.0


def apply_rope(t, cos, sin):
    x1, x2 = np.split(t, 2, axis=-1)
    c = cos[None, None, :, :]
    s = sin[None, None, :, :]
    return np.concatenate([x1 * c - x2 * s, x2 * c + x1 * s], axis=-1)


def draw0():
    s = mx_kscale(E)
    inv_freq = 1.0 / THETA ** (np.arange(0, HD, 2) / HD)
    pos = np.random.randint(0, S) + np.arange(S)
    ang = pos[:, None] * inv_freq[None, :]
    return {"x": bf(np.random.standard_normal((B, S, E)) * s),
            "Wq": bf(np.random.standard_normal((H * HD, E)) * 1.3 / np.sqrt(E) / s[None, :]),
            "bq": bf(np.random.standard_normal(H * HD) * 0.3),
            "Wkv": bf(np.random.standard_normal((2 * KVH * HD, E)) * 1.3 / np.sqrt(E) / s[None, :]),
            "bkv": bf(np.random.standard_normal(2 * KVH * HD) * 0.3),
            "cos": bf(np.cos(ang)),
            "sin": bf(np.sin(ang))}


def core(x, Wq, bq, Wkv, bkv, cos, sin):
    xq = mxq(f64(x), 2, "e4m3")
    q = (xq @ mxq(f64(Wq), 1, "e4m3").T) + f64(bq)
    kv = (xq @ mxq(f64(Wkv), 1, "e4m3").T) + f64(bkv)
    k, v = np.split(kv, 2, axis=-1)
    q = q.reshape(B, S, H, HD).transpose(0, 2, 1, 3)
    k = k.reshape(B, S, KVH, HD).transpose(0, 2, 1, 3)
    v = v.reshape(B, S, KVH, HD).transpose(0, 2, 1, 3)
    q_rot = apply_rope(q, f64(cos), f64(sin))
    k_rot = apply_rope(k, f64(cos), f64(sin))
    return q_rot, k_rot, v


def e4m3fn_bytes(y):
    return np.clip(np.asarray(y, np.float64), -448.0, 448.0).astype(np.float32).astype(ml_dtypes.float8_e4m3fn).view(np.uint8)


def e4m3fn_values(b):
    return np.asarray(b, np.uint8).view(ml_dtypes.float8_e4m3fn).astype(np.float64)


def setup_inputs():
    d = draw0()
    x0 = np.asarray(d['Wq']).astype(np.float64)
    s = (np.max(np.abs(x0), axis=(0,), keepdims=True) / 448.0).astype(np.float32)
    out = {}
    for k, v in d.items():
        if k == 'Wq':
            out['Wq_bytes'] = e4m3fn_bytes(x0 / s.astype(np.float64))
            out['Wq_scale'] = s
        else:
            out[k] = v
    return out


def reference(x, Wq_bytes, Wq_scale, bq, Wkv, bkv, cos, sin):
    return core(x, e4m3fn_values(Wq_bytes) * Wq_scale.astype(np.float64), bq, Wkv, bkv, cos, sin)

@@ -1,0 +1,337 @@
+from contextlib import ExitStack
+
+import concourse.mybir as mybir
+from concourse.masks import make_identity
+
+FLOPS = 2 * 512 * 2048 * 3072
+
+F32 = mybir.dt.float32
+BF16 = mybir.dt.bfloat16
+U32 = mybir.dt.uint32
+U8 = mybir.dt.uint8
+FP8 = mybir.dt.float8_e4m3fn
+FP8X4 = mybir.dt.float8_e4m3fn_x4
+MULT = mybir.AluOpType.mult
+ADD = mybir.AluOpType.add
+
+P = 128
+E = 2048
+NG = 4
+UW = 256
+
+UNITS = (
+    ("q", 0), ("q", 1), ("k", 0), ("q", 2), ("q", 3), ("k", 1),
+    ("q", 4), ("q", 5), ("v", 0), ("q", 6), ("q", 7), ("v", 1),
+)
+CAST_ON_VECTOR = ((0, 0), (0, 1))
+IDENT = mybir.ActivationFunctionType.Identity
+
+
+def tile_qwen2attention_pa_kernel(
+    tc, x, Wq_bytes, Wq_scale, bq, Wkv, bkv, cos, sin, out_0, out_1, out_2
+):
+    nc = tc.nc
+    nu = len(UNITS)
+    xf = x.rearrange("b s k -> (b s) k")
+    outs = {
+        "q": out_0.rearrange("b h s f -> (b h) s f"),
+        "k": out_1.rearrange("b h s f -> (b h) s f"),
+        "v": out_2.rearrange("b h s f -> (b h) s f"),
+    }
+
+    with ExitStack() as ctx:
+        const = ctx.enter_context(tc.tile_pool(name="const", bufs=1))
+        rawp = ctx.enter_context(tc.tile_pool(name="raw", bufs=1))
+        work = ctx.enter_context(tc.tile_pool(name="work", bufs=2))
+        psum = ctx.enter_context(tc.psum_pool(name="psum", bufs=1))
+        ctx.enter_context(tc.manual_schedule())
+
+        raw = {}
+        words = {}
+        tpt = {}
+        grp = {}
+        codes = {}
+        accs = {}
+        eps = {}
+        obs = {}
+
+        ident_f = const.tile([P, P], F32, name="ident_f")
+        make_identity(nc, ident_f[:])
+        ident_b = const.tile([P, P], BF16, name="ident_b")
+        make_identity(nc, ident_b[:])
+        swap_f = const.tile([P, P], F32, name="swap_f")
+        nc.gpsimd.tensor_copy(out=swap_f[:, 0:64], in_=ident_f[:, 64:128])
+        nc.gpsimd.tensor_copy(out=swap_f[:, 64:128], in_=ident_f[:, 0:64])
+
+        warm = const.tile([P, 2], F32, name="warm")
+        nc.vector.memset(warm[:, 0:1], 0.0)
+        nc.scalar.copy(out=warm[:, 1:2], in_=warm[:, 0:1])
+        zb = const.tile([P, P], BF16, name="zb")
+        nc.vector.memset(zb[:], 0.0)
+
+        def load_unit(n, split):
+            kind, a = UNITS[n]
+            if kind == "q":
+                dt, src, nm = U8, Wq_bytes[UW * a:UW * a + UW, :], "wq8_%d" % n
+            else:
+                r0 = UW * a + (512 if kind == "v" else 0)
+                dt, src, nm = BF16, Wkv[r0:r0 + UW, :], "wkv_%d" % n
+            if split:
+                for t in range(2):
+                    tl = rawp.tile([P, E], dt, name="%s_%d" % (nm, t))
+                    nc.sync.dma_start(out=tl[:], in_=src[128 * t:128 * t + 128, :])
+                    raw[(n, t)] = tl[:]
+            else:
+                tl = rawp.tile([P, 2, E], dt, name=nm)
+                nc.sync.dma_start(out=tl[:], in_=src.rearrange("(t p) k -> p t k", p=P))
+                for t in range(2):
+                    raw[(n, t)] = tl[:, t, :]
+
+        load_unit(0, True)
+        scl = const.tile([P, 16], F32, name="scl")
+        nc.sync.dma_start(
+            out=scl[:].rearrange("p (g t) -> p g t", t=4),
+            in_=Wq_scale.rearrange("o (g p t) -> p (o g) t", p=P, t=4),
+        )
+        load_unit(1, True)
+        x_sb = []
+        for i in range(4):
+            xt = rawp.tile([P, E], BF16, name="x_sb%d" % i)
+            nc.sync.dma_start(out=xt[:], in_=xf[128 * i:128 * i + 128, :])
+            x_sb.append(xt)
+        cs_sb = const.tile([P, 4, 2, P], BF16, name="cs_sb")
+        for w in range(2):
+            nc.sync.dma_start(out=cs_sb[:, :, 0, 64 * w:64 * w + 64], in_=cos.rearrange("(i p) j -> p i j", p=P))
+            nc.sync.dma_start(out=cs_sb[:, :, 1, 64 * w:64 * w + 64], in_=sin.rearrange("(i p) j -> p i j", p=P))
+        nc.sync.dma_start(out=zb[0:16, :], in_=bq.rearrange("(h f) -> h f", f=P))
+        nc.sync.dma_start(out=zb[16:24, :], in_=bkv.rearrange("(h f) -> h f", f=P))
+        for n in range(2, nu):
+            load_unit(n, False)
+        bbv = const.tile([P, 512], BF16, name="bbv")
+        nc.sync.dma_start(out=bbv[:], in_=bkv[512:1024].partition_broadcast(P))
+        nc.gpsimd.tensor_scalar(
+            out=cs_sb[:, :, 1, 64:128], in0=cs_sb[:, :, 1, 64:128], scalar1=-1.0, scalar2=0.0, op0=MULT, op1=ADD
+        )
+
+        def cast(n, tiles=(0, 1)):
+            for t in tiles:
+                if UNITS[n][0] == "q":
+                    wb = work.tile([P, E], BF16, name="wb", tag="wb", bufs=6)
+                    if (n, t) in CAST_ON_VECTOR:
+                        nc.vector.tensor_copy(out=wb[:], in_=raw[(n, t)].bitcast(FP8))
+                    else:
+                        nc.scalar.copy(out=wb[:], in_=raw[(n, t)].bitcast(FP8))
+                    words[(n, t)] = wb[:].bitcast(F32)
+                else:
+                    wpk = work.tile([P, 1024], F32, name="wpk", tag="wpk", bufs=4)
+                    nc.scalar.copy(
+                        out=wpk[:].rearrange("p (g u w) -> p g u w", g=4, u=2),
+                        in_=raw[(n, t)].bitcast(F32).rearrange("p (g w u) -> p g u w", g=4, u=2),
+                    )
+                    words[(n, t)] = wpk[:]
+
+        def transpose_bank(w2, g, bank, ordered=False):
+            tp = psum.tile([P, 512], F32, name=bank, tag=bank)
+            for t in range(2):
+                for u in range(2):
+                    c0 = 256 * u + 128 * t
+                    if ordered:
+                        src = w2[t][:, 256 * g + 128 * u:256 * g + 128 * u + 128]
+                    else:
+                        src = w2[t][:, 256 * g + u:256 * (g + 1):2]
+                    nc.tensor.transpose(tp[:, c0:c0 + 128], src, ident_f[:])
+            return tp
+
+        def new_grp():
+            return work.tile([P, 4 * 1024], BF16, name="grp", tag="grp", bufs=3, align_bytes=64)
+
+        def copy_out_plain(tp, gt, c0):
+            nc.scalar.copy(
+                out=gt[:, c0:c0 + 1024].bitcast(F32).rearrange("p (r u) -> p r u", u=2),
+                in_=tp[:].rearrange("p (u r) -> p r u", u=2),
+            )
+
+        def copy_out_scaled(tp, gt, g):
+            nc.vector.tensor_tensor(
+                out=gt[:, 1024 * g:1024 * (g + 1)].rearrange("p (r u e) -> p r u e", u=2, e=2),
+                in0=tp[:].bitcast(BF16).rearrange("p (u r e) -> p r u e", u=2, e=2),
+                in1=scl[:, 4 * g:4 * g + 4].rearrange("p (o u e) -> p o u e", o=1, u=2).to_broadcast([P, 256, 2, 2]),
+                op=MULT,
+            )
+
+        def tr(n, g):
+            tpt[(n, g)] = transpose_bank((words[(n, 0)], words[(n, 1)]), g, "tp%d" % g, UNITS[n][0] != "q")
+            if UNITS[n][0] != "q":
+                if g == 0:
+                    grp[n] = new_grp()
+                copy_out_plain(tpt[(n, g)], grp[n], 1024 * g)
+
+        def co(n, g):
+            if UNITS[n][0] == "q":
+                if g == 0:
+                    grp[n] = new_grp()
+                copy_out_scaled(tpt[(n, g)], grp[n], g)
+
+        def quantize(gt, c, s):
+            nc.vector.quantize_mx(out=c[:].bitcast(FP8X4), scales=s[:], in_=gt[:])
+
+        def qz(n):
+            c = work.tile([P, 1024], U32, name="wc", tag="wc", bufs=3, align_bytes=64)
+            s = work.tile([P, 1024], U8, name="ws", tag="ws", bufs=3, align_bytes=64)
+            quantize(grp[n], c, s)
+            codes[n] = (c, s)
+
+        def head_of(n, hh):
+            kind, a = UNITS[n]
+            return 2 * a + hh + (0 if kind == "q" else (16 if kind == "k" else 20))
+
+        def mm_ev(n, hh):
+            c, s = codes[n]
+            acc = psum.tile([P, 512], F32, name="ac%d" % hh, tag="ac%d" % hh)
+            for g in range(NG):
+                wcol = slice(256 * g + 128 * hh, 256 * g + 128 * hh + 128)
+                xcol = slice(512 * (g % 2), 512 * (g % 2) + 512)
+                nc.tensor.matmul_mx(
+                    out=acc[:],
+                    lhsT=c[:, wcol].bitcast(FP8X4),
+                    lhsT_scale=s[:, wcol],
+                    rhs=xc[g // 2][:, xcol].bitcast(FP8X4),
+                    rhs_scale=xs[g // 2][:, xcol],
+                    start=(g == 0),
+                    stop=(g == NG - 1),
+                )
+            h = head_of(n, hh)
+            av = work.tile([P, 512], F32, name="av", tag="av", bufs=4)
+            nc.scalar.activation(out=av[:], in_=acc[:], func=IDENT, bias=bcol[:, h:h + 1], scale=1.0)
+            if UNITS[n][0] == "v":
+                eps[(n, hh)] = av
+            else:
+                t12 = work.tile([P, 1024], F32, name="t12", tag="t12", bufs=6)
+                nc.gpsimd.tensor_tensor(
+                    out=t12[:].rearrange("p (z c) -> p z c", z=2),
+                    in0=av[:].rearrange("p (o c) -> p o c", o=1).to_broadcast([P, 2, 512]),
+                    in1=tbT[:].rearrange("p (z c) -> p z c", z=2),
+                    op=MULT,
+                )
+                eps[(n, hh)] = t12
+
+        def mm_v(n, ip):
+            c, s = codes[n]
+            acc = psum.tile([P, 512], F32, name="ac%d" % ip, tag="ac%d" % ip)
+            for il in range(2):
+                for g in range(NG):
+                    x0 = 512 * (g % 2) + 128 * (2 * ip + il)
+                    wcol = slice(256 * g, 256 * g + 256)
+                    nc.tensor.matmul_mx(
+                        out=acc[:, 256 * il:256 * il + 256],
+                        lhsT=xc[g // 2][:, x0:x0 + 128].bitcast(FP8X4),
+                        lhsT_scale=xs[g // 2][:, x0:x0 + 128],
+                        rhs=c[:, wcol].bitcast(FP8X4),
+                        rhs_scale=s[:, wcol],
+                        start=(g == 0),
+                        stop=(g == NG - 1),
+                    )
+            accs[(n, ip)] = acc
+
+        def fin_v(n, ip):
+            a = UNITS[n][1]
+            o = work.tile([P, 512], F32, name="o", tag="o", bufs=4)
+            nc.vector.tensor_tensor(
+                out=o[:].rearrange("p (i f) -> p i f", i=2),
+                in0=accs[(n, ip)][:].rearrange("p (i f) -> p i f", i=2),
+                in1=bbv[:, UW * a:UW * a + UW].rearrange("p (o f) -> p o f", o=1).to_broadcast([P, 2, UW]),
+                op=ADD,
+            )
+            for il in range(2):
+                i = 2 * ip + il
+                nc.sync.dma_start(
+                    out=outs["v"][2 * a:2 * a + 2, 128 * i:128 * i + 128, :].rearrange("h p f -> p h f"),
+                    in_=o[:, 256 * il:256 * il + 256].rearrange("p (h f) -> p h f", h=2),
+                )
+
+        def bt(n, hh):
+            kind, a = UNITS[n]
+            t = eps[(n, hh)]
+            ob = psum.tile([P, 512], F32, name="ob%d" % hh, tag="ob%d" % hh)
+            for i in range(4):
+                col = slice(128 * i, 128 * i + 128)
+                if kind == "v":
+                    nc.tensor.transpose(ob[:, col], t[:, col], ident_f[:])
+                else:
+                    nc.tensor.matmul(out=ob[:, col], lhsT=t[:, col], rhs=ident_f[:], is_transpose=True, start=True, stop=False)
+                    nc.tensor.matmul(
+                        out=ob[:, col], lhsT=t[:, 512 + 128 * i:640 + 128 * i], rhs=swap_f[:],
+                        is_transpose=True, start=False, stop=True,
+                    )
+            obs[(n, hh)] = ob
+
+        def fin(n, hh):
+            kind, a = UNITS[n]
+            o = work.tile([P, 512], F32, name="o", tag="o", bufs=4)
+            if hh == 0:
+                nc.vector.tensor_copy(out=o[:], in_=obs[(n, hh)][:])
+            else:
+                nc.scalar.copy(out=o[:], in_=obs[(n, hh)][:])
+            nc.sync.dma_start(
+                out=outs[kind][2 * a + hh, :, :].rearrange("(i p) f -> p i f", p=P),
+                in_=o[:].rearrange("p (i f) -> p i f", i=4),
+            )
+
+        cast(0)
+        cast(1)
+        for g in range(NG):
+            tr(0, g)
+        xc = []
+        xs = []
+        xg = []
+        xbanks = ("ac0", "ac1", "ob0", "ob1")
+        for gp in range(2):
+            gt = new_grp()
+            for k in range(4):
+                g, ip = 2 * gp + k // 2, k % 2
+                tp = transpose_bank((x_sb[2 * ip][:].bitcast(F32), x_sb[2 * ip + 1][:].bitcast(F32)), g, xbanks[k])
+                copy_out_plain(tp, gt, 2048 * (k // 2) + 1024 * ip)
+            xg.append(gt)
+        bcol = const.tile([P, 24], F32, name="bcol")
+        tbT = const.tile([P, 1024], BF16, name="tbT")
+
+        for s in range(-1, nu + 1):
+            for half in range(2):
+                if 0 <= s < nu:
+                    if UNITS[s][0] == "v":
+                        mm_v(s, half)
+                    else:
+                        mm_ev(s, half)
+                if s + 3 < nu:
+                    cast(s + 3, (half,))
+                for g in (2 * half, 2 * half + 1):
+                    if s + 1 < nu:
+                        co(s + 1, g)
+                    if s + 2 < nu:
+                        tr(s + 2, g)
+                if s >= 1 and UNITS[s - 1][0] != "v":
+                    bt(s - 1, half)
+            if s == -1:
+                zt_ps = psum.tile([P, P], BF16, name="ob0", tag="ob0")
+                nc.tensor.transpose(zt_ps[:], zb[:], ident_b[:])
+                nc.scalar.copy(out=bcol[:], in_=zt_ps[:, 0:24])
+                tb_ps = psum.tile([P, 1024], BF16, name="ob1", tag="ob1")
+                for z in range(2):
+                    for i in range(4):
+                        nc.tensor.transpose(tb_ps[:, 512 * z + 128 * i:512 * z + 128 * i + 128], cs_sb[:, i, z, :], ident_b[:])
+                nc.scalar.copy(out=tbT[:], in_=tb_ps[:])
+            if s + 1 < nu:
+                qz(s + 1)
+            if s == -1:
+                for gp in range(2):
+                    c = const.tile([P, 1024], U32, name="xc%d" % gp, align_bytes=64)
+                    sc = const.tile([P, 1024], U8, name="xs%d" % gp, align_bytes=64)
+                    quantize(xg[gp], c, sc)
+                    xc.append(c)
+                    xs.append(sc)
+            if 0 <= s < nu and UNITS[s][0] == "v":
+                fin_v(s, 0)
+                fin_v(s, 1)
+            if s >= 1 and UNITS[s - 1][0] != "v":
+                fin(s - 1, 0)
+                fin(s - 1, 1)

@@ -268,10 +268,7 @@ def tile_qwen2attention_pa_kernel(
         def fin(n, hh):
             kind, a = UNITS[n]
             o = work.tile([P, 512], F32, name="o", tag="o", bufs=4)
-            if hh == 0:
-                nc.vector.tensor_copy(out=o[:], in_=obs[(n, hh)][:])
-            else:
-                nc.scalar.copy(out=o[:], in_=obs[(n, hh)][:])
+            nc.scalar.copy(out=o[:], in_=obs[(n, hh)][:])
             nc.sync.dma_start(
                 out=outs[kind][2 * a + hh, :, :].rearrange("(i p) f -> p i f", p=P),
                 in_=o[:].rearrange("p (i f) -> p i f", i=4),

@@ -20,8 +20,7 @@ NG = 4
 UW = 256
 
 UNITS = (
-    ("q", 0), ("q", 1), ("k", 0), ("q", 2), ("q", 3), ("k", 1),
-    ("q", 4), ("q", 5), ("v", 0), ("q", 6), ("q", 7), ("v", 1),
+    ("q", 0), ("q", 1), ("k", 0), ("q", 2), ("q", 3), ("k", 1), ("q", 4), ("q", 5), ("q", 6), ("q", 7), ("v", 0), ("v", 1),
 )
 CAST_ON_VECTOR = ((0, 0), (0, 1))
 IDENT = mybir.ActivationFunctionType.Identity

@@ -13,6 +13,7 @@ FP8 = mybir.dt.float8_e4m3fn
 FP8X4 = mybir.dt.float8_e4m3fn_x4
 MULT = mybir.AluOpType.mult
 ADD = mybir.AluOpType.add
+IDENT = mybir.ActivationFunctionType.Identity
 
 P = 128
 E = 2048
@@ -20,10 +21,13 @@ NG = 4
 UW = 256
 
 UNITS = (
-    ("q", 0), ("q", 1), ("k", 0), ("q", 2), ("q", 3), ("k", 1), ("q", 4), ("q", 5), ("q", 6), ("q", 7), ("v", 0), ("v", 1),
+    ("q", 0), ("k", 0), ("q", 1), ("q", 2), ("k", 1), ("q", 3),
+    ("q", 4), ("q", 5), ("q", 6), ("q", 7), ("v", 0), ("v", 1),
 )
-CAST_ON_VECTOR = ((0, 0), (0, 1))
-IDENT = mybir.ActivationFunctionType.Identity
+LOADS = (0, "scl", "x", 2, 1, "small")
+KV_AS_LOADED = (1,)
+Q_ORDERED = ()
+CHUNKED = (0,)
 
 
 def tile_qwen2attention_pa_kernel(
@@ -68,81 +72,99 @@ def tile_qwen2attention_pa_kernel(
         zb = const.tile([P, P], BF16, name="zb")
         nc.vector.memset(zb[:], 0.0)
 
-        def load_unit(n, split):
+        def load_unit(n):
             kind, a = UNITS[n]
             if kind == "q":
                 dt, src, nm = U8, Wq_bytes[UW * a:UW * a + UW, :], "wq8_%d" % n
             else:
                 r0 = UW * a + (512 if kind == "v" else 0)
                 dt, src, nm = BF16, Wkv[r0:r0 + UW, :], "wkv_%d" % n
-            if split:
-                for t in range(2):
-                    tl = rawp.tile([P, E], dt, name="%s_%d" % (nm, t))
-                    nc.sync.dma_start(out=tl[:], in_=src[128 * t:128 * t + 128, :])
-                    raw[(n, t)] = tl[:]
+            tl = rawp.tile([P, 2, E], dt, name=nm)
+            view = src.rearrange("(t p) k -> p t k", p=P)
+            if n in CHUNKED:
+                for g in range(NG):
+                    nc.sync.dma_start(out=tl[:, :, 512 * g:512 * g + 512], in_=view[:, :, 512 * g:512 * g + 512])
             else:
-                tl = rawp.tile([P, 2, E], dt, name=nm)
-                nc.sync.dma_start(out=tl[:], in_=src.rearrange("(t p) k -> p t k", p=P))
-                for t in range(2):
-                    raw[(n, t)] = tl[:, t, :]
+                nc.sync.dma_start(out=tl[:], in_=view)
+            for t in range(2):
+                raw[(n, t)] = tl[:, t, :]
 
-        load_unit(0, True)
         scl = const.tile([P, 16], F32, name="scl")
-        nc.sync.dma_start(
-            out=scl[:].rearrange("p (g t) -> p g t", t=4),
-            in_=Wq_scale.rearrange("o (g p t) -> p (o g) t", p=P, t=4),
-        )
-        load_unit(1, True)
         x_sb = []
-        for i in range(4):
-            xt = rawp.tile([P, E], BF16, name="x_sb%d" % i)
-            nc.sync.dma_start(out=xt[:], in_=xf[128 * i:128 * i + 128, :])
-            x_sb.append(xt)
         cs_sb = const.tile([P, 4, 2, P], BF16, name="cs_sb")
-        for w in range(2):
-            nc.sync.dma_start(out=cs_sb[:, :, 0, 64 * w:64 * w + 64], in_=cos.rearrange("(i p) j -> p i j", p=P))
-            nc.sync.dma_start(out=cs_sb[:, :, 1, 64 * w:64 * w + 64], in_=sin.rearrange("(i p) j -> p i j", p=P))
-        nc.sync.dma_start(out=zb[0:16, :], in_=bq.rearrange("(h f) -> h f", f=P))
-        nc.sync.dma_start(out=zb[16:24, :], in_=bkv.rearrange("(h f) -> h f", f=P))
-        for n in range(2, nu):
-            load_unit(n, False)
+        for item in LOADS + tuple(n for n in range(nu) if n not in LOADS):
+            if item == "scl":
+                nc.sync.dma_start(
+                    out=scl[:].rearrange("p (g t) -> p g t", t=4),
+                    in_=Wq_scale.rearrange("o (g p t) -> p (o g) t", p=P, t=4),
+                )
+            elif item == "x":
+                for i in range(4):
+                    xt = rawp.tile([P, E], BF16, name="x_sb%d" % i)
+                    nc.sync.dma_start(out=xt[:], in_=xf[128 * i:128 * i + 128, :])
+                    x_sb.append(xt)
+            elif item == "small":
+                for w in range(2):
+                    nc.sync.dma_start(out=cs_sb[:, :, 0, 64 * w:64 * w + 64], in_=cos.rearrange("(i p) j -> p i j", p=P))
+                    nc.sync.dma_start(out=cs_sb[:, :, 1, 64 * w:64 * w + 64], in_=sin.rearrange("(i p) j -> p i j", p=P))
+                nc.sync.dma_start(out=zb[0:16, :], in_=bq.rearrange("(h f) -> h f", f=P))
+                nc.sync.dma_start(out=zb[16:24, :], in_=bkv.rearrange("(h f) -> h f", f=P))
+            else:
+                load_unit(item)
         bbv = const.tile([P, 512], BF16, name="bbv")
         nc.sync.dma_start(out=bbv[:], in_=bkv[512:1024].partition_broadcast(P))
         nc.gpsimd.tensor_scalar(
             out=cs_sb[:, :, 1, 64:128], in0=cs_sb[:, :, 1, 64:128], scalar1=-1.0, scalar2=0.0, op0=MULT, op1=ADD
         )
 
-        def cast(n, tiles=(0, 1)):
-            for t in tiles:
-                if UNITS[n][0] == "q":
-                    wb = work.tile([P, E], BF16, name="wb", tag="wb", bufs=6)
-                    if (n, t) in CAST_ON_VECTOR:
-                        nc.vector.tensor_copy(out=wb[:], in_=raw[(n, t)].bitcast(FP8))
-                    else:
-                        nc.scalar.copy(out=wb[:], in_=raw[(n, t)].bitcast(FP8))
-                    words[(n, t)] = wb[:].bitcast(F32)
-                else:
-                    wpk = work.tile([P, 1024], F32, name="wpk", tag="wpk", bufs=4)
-                    nc.scalar.copy(
-                        out=wpk[:].rearrange("p (g u w) -> p g u w", g=4, u=2),
-                        in_=raw[(n, t)].bitcast(F32).rearrange("p (g w u) -> p g u w", g=4, u=2),
-                    )
-                    words[(n, t)] = wpk[:]
+        def put_in_order(src_words, tag):
+            wpk = work.tile([P, 1024], F32, name=tag, tag=tag, bufs=4)
+            nc.scalar.copy(
+                out=wpk[:].rearrange("p (g u w) -> p g u w", g=4, u=2),
+                in_=src_words.rearrange("p (g w u) -> p g u w", g=4, u=2),
+            )
+            return wpk[:]
 
-        def transpose_bank(w2, g, bank, ordered=False):
+        def cast(n, tiles=(0, 1)):
+            if UNITS[n][0] != "q":
+                for t in tiles:
+                    if n in KV_AS_LOADED:
+                        words[(n, t)] = (raw[(n, t)].bitcast(F32), False)
+                    else:
+                        words[(n, t)] = (put_in_order(raw[(n, t)].bitcast(F32), "wpk"), True)
+                return
+            wbs = {}
+            for t in tiles:
+                wbs[t] = work.tile([P, E], BF16, name="wb", tag="wb", bufs=6)
+            if n in CHUNKED:
+                for g in range(NG):
+                    for t in tiles:
+                        col = slice(512 * g, 512 * g + 512)
+                        nc.scalar.copy(out=wbs[t][:, col], in_=raw[(n, t)][:, col].bitcast(FP8))
+            else:
+                for t in tiles:
+                    nc.scalar.copy(out=wbs[t][:], in_=raw[(n, t)].bitcast(FP8))
+            for t in tiles:
+                if (n, t) in Q_ORDERED:
+                    words[(n, t)] = (put_in_order(wbs[t][:].bitcast(F32), "wpq"), True)
+                else:
+                    words[(n, t)] = (wbs[t][:].bitcast(F32), False)
+
+        def transpose_bank(w2, g, bank):
             tp = psum.tile([P, 512], F32, name=bank, tag=bank)
             for t in range(2):
+                w, ordered = w2[t]
                 for u in range(2):
                     c0 = 256 * u + 128 * t
                     if ordered:
-                        src = w2[t][:, 256 * g + 128 * u:256 * g + 128 * u + 128]
+                        src = w[:, 256 * g + 128 * u:256 * g + 128 * u + 128]
                     else:
-                        src = w2[t][:, 256 * g + u:256 * (g + 1):2]
+                        src = w[:, 256 * g + u:256 * (g + 1):2]
                     nc.tensor.transpose(tp[:, c0:c0 + 128], src, ident_f[:])
             return tp
 
         def new_grp():
-            return work.tile([P, 4 * 1024], BF16, name="grp", tag="grp", bufs=3, align_bytes=64)
+            return work.tile([P, 4 * 1024], BF16, name="grp", tag="grp", bufs=4, align_bytes=64)
 
         def copy_out_plain(tp, gt, c0):
             nc.scalar.copy(
@@ -159,7 +181,7 @@ def tile_qwen2attention_pa_kernel(
             )
 
         def tr(n, g):
-            tpt[(n, g)] = transpose_bank((words[(n, 0)], words[(n, 1)]), g, "tp%d" % g, UNITS[n][0] != "q")
+            tpt[(n, g)] = transpose_bank((words[(n, 0)], words[(n, 1)]), g, "tp%d" % g)
             if UNITS[n][0] != "q":
                 if g == 0:
                     grp[n] = new_grp()
@@ -182,7 +204,7 @@ def tile_qwen2attention_pa_kernel(
 
         def head_of(n, hh):
             kind, a = UNITS[n]
-            return 2 * a + hh + (0 if kind == "q" else (16 if kind == "k" else 20))
+            return 2 * a + hh + (0 if kind == "q" else 16)
 
         def mm_ev(n, hh):
             c, s = codes[n]
@@ -202,17 +224,14 @@ def tile_qwen2attention_pa_kernel(
             h = head_of(n, hh)
             av = work.tile([P, 512], F32, name="av", tag="av", bufs=4)
             nc.scalar.activation(out=av[:], in_=acc[:], func=IDENT, bias=bcol[:, h:h + 1], scale=1.0)
-            if UNITS[n][0] == "v":
-                eps[(n, hh)] = av
-            else:
-                t12 = work.tile([P, 1024], F32, name="t12", tag="t12", bufs=6)
-                nc.gpsimd.tensor_tensor(
-                    out=t12[:].rearrange("p (z c) -> p z c", z=2),
-                    in0=av[:].rearrange("p (o c) -> p o c", o=1).to_broadcast([P, 2, 512]),
-                    in1=tbT[:].rearrange("p (z c) -> p z c", z=2),
-                    op=MULT,
-                )
-                eps[(n, hh)] = t12
+            t12 = work.tile([P, 1024], F32, name="t12", tag="t12", bufs=4)
+            nc.gpsimd.tensor_tensor(
+                out=t12[:].rearrange("p (z c) -> p z c", z=2),
+                in0=av[:].rearrange("p (o c) -> p o c", o=1).to_broadcast([P, 2, 512]),
+                in1=tbT[:].rearrange("p (z c) -> p z c", z=2),
+                op=MULT,
+            )
+            eps[(n, hh)] = t12
 
         def mm_v(n, ip):
             c, s = codes[n]
@@ -249,19 +268,15 @@ def tile_qwen2attention_pa_kernel(
                 )
 
         def bt(n, hh):
-            kind, a = UNITS[n]
             t = eps[(n, hh)]
             ob = psum.tile([P, 512], F32, name="ob%d" % hh, tag="ob%d" % hh)
             for i in range(4):
                 col = slice(128 * i, 128 * i + 128)
-                if kind == "v":
-                    nc.tensor.transpose(ob[:, col], t[:, col], ident_f[:])
-                else:
-                    nc.tensor.matmul(out=ob[:, col], lhsT=t[:, col], rhs=ident_f[:], is_transpose=True, start=True, stop=False)
-                    nc.tensor.matmul(
-                        out=ob[:, col], lhsT=t[:, 512 + 128 * i:640 + 128 * i], rhs=swap_f[:],
-                        is_transpose=True, start=False, stop=True,
-                    )
+                nc.tensor.matmul(out=ob[:, col], lhsT=t[:, col], rhs=ident_f[:], is_transpose=True, start=True, stop=False)
+                nc.tensor.matmul(
+                    out=ob[:, col], lhsT=t[:, 512 + 128 * i:640 + 128 * i], rhs=swap_f[:],
+                    is_transpose=True, start=False, stop=True,
+                )
             obs[(n, hh)] = ob
 
         def fin(n, hh):
@@ -274,20 +289,17 @@ def tile_qwen2attention_pa_kernel(
             )
 
         cast(0)
-        cast(1)
         for g in range(NG):
             tr(0, g)
         xc = []
         xs = []
-        xg = []
+        xg = [new_grp(), new_grp()]
         xbanks = ("ac0", "ac1", "ob0", "ob1")
-        for gp in range(2):
-            gt = new_grp()
-            for k in range(4):
-                g, ip = 2 * gp + k // 2, k % 2
-                tp = transpose_bank((x_sb[2 * ip][:].bitcast(F32), x_sb[2 * ip + 1][:].bitcast(F32)), g, xbanks[k])
-                copy_out_plain(tp, gt, 2048 * (k // 2) + 1024 * ip)
-            xg.append(gt)
+        for ip in range(2):
+            for g in range(NG):
+                tp = transpose_bank(((x_sb[2 * ip][:].bitcast(F32), False), (x_sb[2 * ip + 1][:].bitcast(F32), False)), g, xbanks[g])
+                copy_out_plain(tp, xg[g // 2], 2048 * (g % 2) + 1024 * ip)
+        cast(1)
         bcol = const.tile([P, 24], F32, name="bcol")
         tbT = const.tile([P, 1024], BF16, name="tbT")
 

@@ -27,6 +27,7 @@ UNITS = (
 LOADS = (0, "scl", "x", 2, 1, "small")
 KV_AS_LOADED = (1,)
 Q_ORDERED = ()
+Q_ON_VECTOR = (3,)
 CHUNKED = (0,)
 
 
@@ -69,6 +70,8 @@ def tile_qwen2attention_pa_kernel(
         warm = const.tile([P, 2], F32, name="warm")
         nc.vector.memset(warm[:, 0:1], 0.0)
         nc.scalar.copy(out=warm[:, 1:2], in_=warm[:, 0:1])
+        ones = const.tile([P, 1], F32, name="ones")
+        nc.vector.memset(ones[:], 1.0)
         zb = const.tile([P, P], BF16, name="zb")
         nc.vector.memset(zb[:], 0.0)
 
@@ -136,6 +139,15 @@ def tile_qwen2attention_pa_kernel(
             wbs = {}
             for t in tiles:
                 wbs[t] = work.tile([P, E], BF16, name="wb", tag="wb", bufs=6)
+            if n in Q_ON_VECTOR:
+                for t in tiles:
+                    nc.vector.tensor_scalar(
+                        out=wbs[t][:].rearrange("p (u w e) -> p w u e", u=2, e=2),
+                        in0=raw[(n, t)].bitcast(FP8).rearrange("p (w u e) -> p w u e", u=2, e=2),
+                        scalar1=ones[:, 0:1], scalar2=None, op0=MULT,
+                    )
+                    words[(n, t)] = (wbs[t][:].bitcast(F32), "ugp")
+                return
             if n in CHUNKED:
                 for g in range(NG):
                     for t in tiles:
@@ -156,7 +168,9 @@ def tile_qwen2attention_pa_kernel(
                 w, ordered = w2[t]
                 for u in range(2):
                     c0 = 256 * u + 128 * t
-                    if ordered:
+                    if ordered == "ugp":
+                        src = w[:, 512 * u + 128 * g:512 * u + 128 * g + 128]
+                    elif ordered:
                         src = w[:, 256 * g + 128 * u:256 * g + 128 * u + 128]
                     else:
                         src = w[:, 256 * g + u:256 * (g + 1):2]

@@ -82,13 +82,15 @@ def tile_qwen2attention_pa_kernel(
             else:
                 r0 = UW * a + (512 if kind == "v" else 0)
                 dt, src, nm = BF16, Wkv[r0:r0 + UW, :], "wkv_%d" % n
-            tl = rawp.tile([P, 2, E], dt, name=nm)
             view = src.rearrange("(t p) k -> p t k", p=P)
             if n in CHUNKED:
+                tl = rawp.tile([P, NG, 2, 512], dt, name=nm)
                 for g in range(NG):
-                    nc.sync.dma_start(out=tl[:, :, 512 * g:512 * g + 512], in_=view[:, :, 512 * g:512 * g + 512])
-            else:
-                nc.sync.dma_start(out=tl[:], in_=view)
+                    nc.sync.dma_start(out=tl[:, g, :, :], in_=view[:, :, 512 * g:512 * g + 512])
+                raw[n] = tl
+                return
+            tl = rawp.tile([P, 2, E], dt, name=nm)
+            nc.sync.dma_start(out=tl[:], in_=view)
             for t in range(2):
                 raw[(n, t)] = tl[:, t, :]
 
@@ -136,6 +138,16 @@ def tile_qwen2attention_pa_kernel(
                     else:
                         words[(n, t)] = (put_in_order(raw[(n, t)].bitcast(F32), "wpk"), True)
                 return
+            if n in CHUNKED:
+                wbc = work.tile([P, NG, 2, 512], BF16, name="wbc", tag="wbc", bufs=1)
+                for g in range(NG):
+                    nc.scalar.copy(
+                        out=wbc[:, g, :, :].rearrange("p t k -> p (t k)"),
+                        in_=raw[n][:, g, :, :].rearrange("p t k -> p (t k)").bitcast(FP8),
+                    )
+                for t in tiles:
+                    words[(n, t)] = (wbc[:, :, t, :], "chunks")
+                return
             wbs = {}
             for t in tiles:
                 wbs[t] = work.tile([P, E], BF16, name="wb", tag="wb", bufs=6)
@@ -148,14 +160,8 @@ def tile_qwen2attention_pa_kernel(
                     )
                     words[(n, t)] = (wbs[t][:].bitcast(F32), "ugp")
                 return
-            if n in CHUNKED:
-                for g in range(NG):
-                    for t in tiles:
-                        col = slice(512 * g, 512 * g + 512)
-                        nc.scalar.copy(out=wbs[t][:, col], in_=raw[(n, t)][:, col].bitcast(FP8))
-            else:
-                for t in tiles:
-                    nc.scalar.copy(out=wbs[t][:], in_=raw[(n, t)].bitcast(FP8))
+            for t in tiles:
+                nc.scalar.copy(out=wbs[t][:], in_=raw[(n, t)].bitcast(FP8))
             for t in tiles:
                 if (n, t) in Q_ORDERED:
                     words[(n, t)] = (put_in_order(wbs[t][:].bitcast(F32), "wpq"), True)
@@ -170,6 +176,8 @@ def tile_qwen2attention_pa_kernel(
                     c0 = 256 * u + 128 * t
                     if ordered == "ugp":
                         src = w[:, 512 * u + 128 * g:512 * u + 128 * g + 128]
+                    elif ordered == "chunks":
+                        src = w[:, g, :].bitcast(F32)[:, u:256:2]
                     elif ordered:
                         src = w[:, 256 * g + 128 * u:256 * g + 128 * u + 128]
                     else:
@@ -333,6 +341,8 @@ def tile_qwen2attention_pa_kernel(
                         tr(s + 2, g)
                 if s >= 1 and UNITS[s - 1][0] != "v":
                     bt(s - 1, half)
+                    if half == 0:
+                        fin(s - 1, 0)
             if s == -1:
                 zt_ps = psum.tile([P, P], BF16, name="ob0", tag="ob0")
                 nc.tensor.transpose(zt_ps[:], zb[:], ident_b[:])
@@ -355,5 +365,4 @@ def tile_qwen2attention_pa_kernel(
                 fin_v(s, 0)
                 fin_v(s, 1)
             if s >= 1 and UNITS[s - 1][0] != "v":
-                fin(s - 1, 0)
                 fin(s - 1, 1)

@@ -28,6 +28,7 @@ LOADS = (0, "scl", "x", 2, 1, "small")
 KV_AS_LOADED = (1,)
 Q_ORDERED = ()
 Q_ON_VECTOR = (3,)
+ROPE_ON_VECTOR = (9,)
 CHUNKED = (0,)
 
 
@@ -244,9 +245,19 @@ def tile_qwen2attention_pa_kernel(
                     stop=(g == NG - 1),
                 )
             h = head_of(n, hh)
+            t12 = work.tile([P, 1024], F32, name="t12", tag="t12", bufs=4)
+            eps[(n, hh)] = t12
+            if n in ROPE_ON_VECTOR:
+                nc.vector.scalar_tensor_tensor(
+                    out=t12[:].rearrange("p (z c) -> p z c", z=2),
+                    in0=acc[:].rearrange("p (o c) -> p o c", o=1).to_broadcast([P, 2, 512]),
+                    scalar=bcol[:, h:h + 1],
+                    in1=tbT[:].rearrange("p (z c) -> p z c", z=2),
+                    op0=ADD, op1=MULT,
+                )
+                return
             av = work.tile([P, 512], F32, name="av", tag="av", bufs=4)
             nc.scalar.activation(out=av[:], in_=acc[:], func=IDENT, bias=bcol[:, h:h + 1], scale=1.0)
-            t12 = work.tile([P, 1024], F32, name="t12", tag="t12", bufs=4)
             nc.gpsimd.tensor_tensor(
                 out=t12[:].rearrange("p (z c) -> p z c", z=2),
                 in0=av[:].rearrange("p (o c) -> p o c", o=1).to_broadcast([P, 2, 512]),
@@ -326,6 +337,8 @@ def tile_qwen2attention_pa_kernel(
         tbT = const.tile([P, 1024], BF16, name="tbT")
 
         for s in range(-1, nu + 1):
+            if s in ROPE_ON_VECTOR:
+                qz(s + 1)
             for half in range(2):
                 if 0 <= s < nu:
                     if UNITS[s][0] == "v":
@@ -352,7 +365,7 @@ def tile_qwen2attention_pa_kernel(
                     for i in range(4):
                         nc.tensor.transpose(tb_ps[:, 512 * z + 128 * i:512 * z + 128 * i + 128], cs_sb[:, i, z, :], ident_b[:])
                 nc.scalar.copy(out=tbT[:], in_=tb_ps[:])
-            if s + 1 < nu:
+            if s + 1 < nu and s not in ROPE_ON_VECTOR:
                 qz(s + 1)
             if s == -1:
                 for gp in range(2):

@@ -174,7 +174,6 @@ def tile_qwen2attention_pa_kernel(
             for t in range(2):
                 w, ordered = w2[t]
                 for u in range(2):
-                    c0 = 256 * u + 128 * t
                     if ordered == "ugp":
                         src = w[:, 512 * u + 128 * g:512 * u + 128 * g + 128]
                     elif ordered == "chunks":
@@ -183,7 +182,7 @@ def tile_qwen2attention_pa_kernel(
                         src = w[:, 256 * g + 128 * u:256 * g + 128 * u + 128]
                     else:
                         src = w[:, 256 * g + u:256 * (g + 1):2]
-                    nc.tensor.transpose(tp[:, c0:c0 + 128], src, ident_f[:])
+                    nc.tensor.transpose(tp[:, 256 * t + u:256 * t + 256:2], src, ident_f[:])
             return tp
 
         def new_grp():
@@ -191,15 +190,15 @@ def tile_qwen2attention_pa_kernel(
 
         def copy_out_plain(tp, gt, c0):
             nc.scalar.copy(
-                out=gt[:, c0:c0 + 1024].bitcast(F32).rearrange("p (r u) -> p r u", u=2),
-                in_=tp[:].rearrange("p (u r) -> p r u", u=2),
+                out=gt[:, c0:c0 + 1024].bitcast(F32),
+                in_=tp[:],
             )
 
         def copy_out_scaled(tp, gt, g):
             nc.vector.tensor_tensor(
-                out=gt[:, 1024 * g:1024 * (g + 1)].rearrange("p (r u e) -> p r u e", u=2, e=2),
-                in0=tp[:].bitcast(BF16).rearrange("p (u r e) -> p r u e", u=2, e=2),
-                in1=scl[:, 4 * g:4 * g + 4].rearrange("p (o u e) -> p o u e", o=1, u=2).to_broadcast([P, 256, 2, 2]),
+                out=gt[:, 1024 * g:1024 * (g + 1)].rearrange("p (r t) -> p r t", t=4),
+                in0=tp[:].bitcast(BF16).rearrange("p (r t) -> p r t", t=4),
+                in1=scl[:, 4 * g:4 * g + 4].rearrange("p (o t) -> p o t", o=1).to_broadcast([P, 256, 4]),
                 op=MULT,
             )
 

@@ -21,14 +21,15 @@ NG = 4
 UW = 256
 
 UNITS = (
-    ("q", 0), ("k", 0), ("q", 1), ("q", 2), ("k", 1), ("q", 3),
-    ("q", 4), ("q", 5), ("q", 6), ("q", 7), ("v", 0), ("v", 1),
+    ("q", 0), ("k", 0), ("q", 1), ("q", 2), ("q", 3), ("q", 4),
+    ("q", 5), ("q", 6), ("q", 7), ("k", 1), ("v", 0), ("v", 1),
 )
 LOADS = (0, "scl", "x", 2, 1, "small")
 KV_AS_LOADED = (1,)
 Q_ORDERED = ()
-Q_ON_VECTOR = (3,)
-ROPE_ON_VECTOR = (9,)
+Q_ON_VECTOR = ()
+V_HEADS = ((8, 0), (8, 1), (9, 0), (9, 1))
+Q_EARLY = (8, 9)
 CHUNKED = (0,)
 
 
@@ -243,10 +244,15 @@ def tile_qwen2attention_pa_kernel(
                     start=(g == 0),
                     stop=(g == NG - 1),
                 )
-            h = head_of(n, hh)
-            t12 = work.tile([P, 1024], F32, name="t12", tag="t12", bufs=4)
-            eps[(n, hh)] = t12
-            if n in ROPE_ON_VECTOR:
+            accs[(n, hh)] = acc
+            if (n, hh) not in V_HEADS:
+                rope_g(n, hh)
+
+        def rope_v(n, hh):
+                acc = accs[(n, hh)]
+                h = head_of(n, hh)
+                t12 = work.tile([P, 1024], F32, name="t12", tag="t12", bufs=4)
+                eps[(n, hh)] = t12
                 nc.vector.scalar_tensor_tensor(
                     out=t12[:].rearrange("p (z c) -> p z c", z=2),
                     in0=acc[:].rearrange("p (o c) -> p o c", o=1).to_broadcast([P, 2, 512]),
@@ -254,7 +260,11 @@ def tile_qwen2attention_pa_kernel(
                     in1=tbT[:].rearrange("p (z c) -> p z c", z=2),
                     op0=ADD, op1=MULT,
                 )
-                return
+
+        def rope_g(n, hh):
+            acc = accs[(n, hh)]
+            h = head_of(n, hh)
+            t12 = work.tile([P, 1024], F32, name="t12", tag="t12", bufs=4)
             av = work.tile([P, 512], F32, name="av", tag="av", bufs=4)
             nc.scalar.activation(out=av[:], in_=acc[:], func=IDENT, bias=bcol[:, h:h + 1], scale=1.0)
             nc.gpsimd.tensor_tensor(
@@ -336,7 +346,7 @@ def tile_qwen2attention_pa_kernel(
         tbT = const.tile([P, 1024], BF16, name="tbT")
 
         for s in range(-1, nu + 1):
-            if s in ROPE_ON_VECTOR:
+            if s in Q_EARLY:
                 qz(s + 1)
             for half in range(2):
                 if 0 <= s < nu:
@@ -351,6 +361,8 @@ def tile_qwen2attention_pa_kernel(
                         co(s + 1, g)
                     if s + 2 < nu:
                         tr(s + 2, g)
+                if half == 0 and (s, 0) in V_HEADS:
+                    rope_v(s, 0)
                 if s >= 1 and UNITS[s - 1][0] != "v":
                     bt(s - 1, half)
                     if half == 0:
@@ -364,8 +376,10 @@ def tile_qwen2attention_pa_kernel(
                     for i in range(4):
                         nc.tensor.transpose(tb_ps[:, 512 * z + 128 * i:512 * z + 128 * i + 128], cs_sb[:, i, z, :], ident_b[:])
                 nc.scalar.copy(out=tbT[:], in_=tb_ps[:])
-            if s + 1 < nu and s not in ROPE_ON_VECTOR:
+            if s + 1 < nu and s not in Q_EARLY:
                 qz(s + 1)
+            if (s, 1) in V_HEADS:
+                rope_v(s, 1)
             if s == -1:
                 for gp in range(2):
                     c = const.tile([P, 1024], U32, name="xc%d" % gp, align_bytes=64)

@@ -24,12 +24,19 @@ UNITS = (
     ("q", 0), ("k", 0), ("q", 1), ("q", 2), ("q", 3), ("q", 4),
     ("q", 5), ("q", 6), ("q", 7), ("k", 1), ("v", 0), ("v", 1),
 )
-LOADS = (0, "scl", "x", 2, 1, "small")
+LOADS = (0, 'scl', 'x', 1, 2, 'small')
 KV_AS_LOADED = (1,)
 Q_ORDERED = ()
 Q_ON_VECTOR = ()
 V_HEADS = ((8, 0), (8, 1), (9, 0), (9, 1))
 Q_EARLY = (8, 9)
+CS_ONCE = True
+TAB_LATE = True
+VCOPY = (1,)
+XLAG = 1
+XK = ()
+LAG = 1
+STEP_ALL = True
 CHUNKED = (0,)
 
 
@@ -111,17 +118,24 @@ def tile_qwen2attention_pa_kernel(
                     nc.sync.dma_start(out=xt[:], in_=xf[128 * i:128 * i + 128, :])
                     x_sb.append(xt)
             elif item == "small":
-                for w in range(2):
+                for w in range(1 if CS_ONCE else 2):
                     nc.sync.dma_start(out=cs_sb[:, :, 0, 64 * w:64 * w + 64], in_=cos.rearrange("(i p) j -> p i j", p=P))
                     nc.sync.dma_start(out=cs_sb[:, :, 1, 64 * w:64 * w + 64], in_=sin.rearrange("(i p) j -> p i j", p=P))
                 nc.sync.dma_start(out=zb[0:16, :], in_=bq.rearrange("(h f) -> h f", f=P))
                 nc.sync.dma_start(out=zb[16:24, :], in_=bkv.rearrange("(h f) -> h f", f=P))
             else:
                 load_unit(item)
+        if XK:
+            bbk = const.tile([P, 512], BF16, name="bbk")
+            nc.sync.dma_start(out=bbk[:], in_=bkv[0:512].partition_broadcast(P))
         bbv = const.tile([P, 512], BF16, name="bbv")
         nc.sync.dma_start(out=bbv[:], in_=bkv[512:1024].partition_broadcast(P))
+        if CS_ONCE:
+            nc.gpsimd.tensor_scalar(
+                out=cs_sb[:, :, 0, 64:128], in0=cs_sb[:, :, 0, 0:64], scalar1=1.0, scalar2=0.0, op0=MULT, op1=ADD
+            )
         nc.gpsimd.tensor_scalar(
-            out=cs_sb[:, :, 1, 64:128], in0=cs_sb[:, :, 1, 64:128], scalar1=-1.0, scalar2=0.0, op0=MULT, op1=ADD
+            out=cs_sb[:, :, 1, 64:128], in0=cs_sb[:, :, 1, 0:64] if CS_ONCE else cs_sb[:, :, 1, 64:128], scalar1=-1.0, scalar2=0.0, op0=MULT, op1=ADD
         )
 
         def put_in_order(src_words, tag):
@@ -172,6 +186,7 @@ def tile_qwen2attention_pa_kernel(
 
         def transpose_bank(w2, g, bank):
             tp = psum.tile([P, 512], F32, name=bank, tag=bank)
+            stepped = STEP_ALL or w2[0][1] in (False, "chunks")
             for t in range(2):
                 w, ordered = w2[t]
                 for u in range(2):
@@ -183,29 +198,47 @@ def tile_qwen2attention_pa_kernel(
                         src = w[:, 256 * g + 128 * u:256 * g + 128 * u + 128]
                     else:
                         src = w[:, 256 * g + u:256 * (g + 1):2]
-                    nc.tensor.transpose(tp[:, 256 * t + u:256 * t + 256:2], src, ident_f[:])
-            return tp
+                    c0 = 256 * u + 128 * t
+                    dst = tp[:, 256 * t + u:256 * t + 256:2] if stepped else tp[:, c0:c0 + 128]
+                    nc.tensor.transpose(dst, src, ident_f[:])
+            return tp, stepped
 
         def new_grp():
             return work.tile([P, 4 * 1024], BF16, name="grp", tag="grp", bufs=4, align_bytes=64)
 
-        def copy_out_plain(tp, gt, c0):
-            nc.scalar.copy(
-                out=gt[:, c0:c0 + 1024].bitcast(F32),
-                in_=tp[:],
-            )
+        def by_row(bank):
+            tp, stepped = bank
+            return tp[:].rearrange("p (r u) -> p r u", u=2) if stepped else tp[:].rearrange("p (u r) -> p r u", u=2)
 
-        def copy_out_scaled(tp, gt, g):
+        def copy_out_plain(bank, gt, c0, on_vector=False):
+            dst = gt[:, c0:c0 + 1024].bitcast(F32).rearrange("p (r u) -> p r u", u=2)
+            if on_vector:
+                nc.vector.tensor_copy(out=dst, in_=by_row(bank))
+            else:
+                nc.scalar.copy(out=dst, in_=by_row(bank))
+
+        def copy_out_scaled(bank, gt, g):
+            tp, stepped = bank
+            dst = gt[:, 1024 * g:1024 * (g + 1)]
+            s4 = scl[:, 4 * g:4 * g + 4]
+            if stepped:
+                nc.vector.tensor_tensor(
+                    out=dst.rearrange("p (r t) -> p r t", t=4),
+                    in0=tp[:].bitcast(BF16).rearrange("p (r t) -> p r t", t=4),
+                    in1=s4.rearrange("p (o t) -> p o t", o=1).to_broadcast([P, 256, 4]),
+                    op=MULT,
+                )
+                return
             nc.vector.tensor_tensor(
-                out=gt[:, 1024 * g:1024 * (g + 1)].rearrange("p (r t) -> p r t", t=4),
-                in0=tp[:].bitcast(BF16).rearrange("p (r t) -> p r t", t=4),
-                in1=scl[:, 4 * g:4 * g + 4].rearrange("p (o t) -> p o t", o=1).to_broadcast([P, 256, 4]),
+                out=dst.rearrange("p (r u e) -> p r u e", u=2, e=2),
+                in0=tp[:].bitcast(BF16).rearrange("p (u r e) -> p r u e", u=2, e=2),
+                in1=s4.rearrange("p (o u e) -> p o u e", o=1, u=2).to_broadcast([P, 256, 2, 2]),
                 op=MULT,
             )
 
         def tr(n, g):
             tpt[(n, g)] = transpose_bank((words[(n, 0)], words[(n, 1)]), g, "tp%d" % g)
-            if UNITS[n][0] != "q":
+            if UNITS[n][0] != "q" and n not in VCOPY:
                 if g == 0:
                     grp[n] = new_grp()
                 copy_out_plain(tpt[(n, g)], grp[n], 1024 * g)
@@ -215,6 +248,10 @@ def tile_qwen2attention_pa_kernel(
                 if g == 0:
                     grp[n] = new_grp()
                 copy_out_scaled(tpt[(n, g)], grp[n], g)
+            elif n in VCOPY:
+                if g == 0:
+                    grp[n] = new_grp()
+                copy_out_plain(tpt[(n, g)], grp[n], 1024 * g, True)
 
         def quantize(gt, c, s):
             nc.vector.quantize_mx(out=c[:].bitcast(FP8X4), scales=s[:], in_=gt[:])
@@ -245,13 +282,11 @@ def tile_qwen2attention_pa_kernel(
                     stop=(g == NG - 1),
                 )
             accs[(n, hh)] = acc
-            if (n, hh) not in V_HEADS:
-                rope_g(n, hh)
 
         def rope_v(n, hh):
                 acc = accs[(n, hh)]
                 h = head_of(n, hh)
-                t12 = work.tile([P, 1024], F32, name="t12", tag="t12", bufs=4)
+                t12 = work.tile([P, 1024], F32, name="t12", tag="t12", bufs=2 + 2 * LAG)
                 eps[(n, hh)] = t12
                 nc.vector.scalar_tensor_tensor(
                     out=t12[:].rearrange("p (z c) -> p z c", z=2),
@@ -264,8 +299,8 @@ def tile_qwen2attention_pa_kernel(
         def rope_g(n, hh):
             acc = accs[(n, hh)]
             h = head_of(n, hh)
-            t12 = work.tile([P, 1024], F32, name="t12", tag="t12", bufs=4)
-            av = work.tile([P, 512], F32, name="av", tag="av", bufs=4)
+            t12 = work.tile([P, 1024], F32, name="t12", tag="t12", bufs=2 + 2 * LAG)
+            av = work.tile([P, 512], F32, name="av", tag="av", bufs=2 + 2 * LAG)
             nc.scalar.activation(out=av[:], in_=acc[:], func=IDENT, bias=bcol[:, h:h + 1], scale=1.0)
             nc.gpsimd.tensor_tensor(
                 out=t12[:].rearrange("p (z c) -> p z c", z=2),
@@ -293,6 +328,46 @@ def tile_qwen2attention_pa_kernel(
                     )
             accs[(n, ip)] = acc
 
+        def rope_x(n, ip):
+            a = UNITS[n][1]
+            av = work.tile([P, 512], F32, name="av", tag="av", bufs=2 + 2 * LAG)
+            nc.vector.tensor_tensor(
+                out=av[:].rearrange("p (i f) -> p i f", i=2),
+                in0=accs[(n, ip)][:].rearrange("p (i f) -> p i f", i=2),
+                in1=bbk[:, UW * a:UW * a + UW].rearrange("p (o f) -> p o f", o=1).to_broadcast([P, 2, UW]),
+                op=ADD,
+            )
+            t12 = work.tile([P, 1024], F32, name="t12", tag="t12", bufs=2 + 2 * LAG)
+            for il in range(2):
+                nc.gpsimd.tensor_tensor(
+                    out=t12[:, 512 * il:512 * il + 512].rearrange("p (z h f) -> p z h f", z=2, h=2),
+                    in0=av[:, 256 * il:256 * il + 256].rearrange("p (o h f) -> p o h f", o=1, h=2).to_broadcast([P, 2, 2, P]),
+                    in1=cs_sb[:, 2 * ip + il, :, :].rearrange("p z (o f) -> p z o f", o=1).to_broadcast([P, 2, 2, P]),
+                    op=MULT,
+                )
+            eps[(n, ip)] = t12
+
+        def fin_x(n, ip):
+            a = UNITS[n][1]
+            t = eps[(n, ip)][:].rearrange("p (i z h w f) -> p i z h w f", i=2, z=2, h=2, w=2)
+            o = work.tile([P, 512], F32, name="o", tag="o", bufs=4)
+            for il in range(2):
+                nc.vector.tensor_tensor(
+                    out=o[:, 256 * il:256 * il + 256].rearrange("p (h w f) -> p h w f", h=2, w=2),
+                    in0=t[:, il, 0, :, :, :],
+                    in1=t[:, il, 1, :, ::-1, :],
+                    op=ADD,
+                )
+            store_rows("k", a, ip, o)
+
+        def store_rows(kind, a, ip, o):
+            for il in range(2):
+                i = 2 * ip + il
+                nc.sync.dma_start(
+                    out=outs[kind][2 * a:2 * a + 2, 128 * i:128 * i + 128, :].rearrange("h p f -> p h f"),
+                    in_=o[:, 256 * il:256 * il + 256].rearrange("p (h f) -> p h f", h=2),
+                )
+
         def fin_v(n, ip):
             a = UNITS[n][1]
             o = work.tile([P, 512], F32, name="o", tag="o", bufs=4)
@@ -302,12 +377,7 @@ def tile_qwen2attention_pa_kernel(
                 in1=bbv[:, UW * a:UW * a + UW].rearrange("p (o f) -> p o f", o=1).to_broadcast([P, 2, UW]),
                 op=ADD,
             )
-            for il in range(2):
-                i = 2 * ip + il
-                nc.sync.dma_start(
-                    out=outs["v"][2 * a:2 * a + 2, 128 * i:128 * i + 128, :].rearrange("h p f -> p h f"),
-                    in_=o[:, 256 * il:256 * il + 256].rearrange("p (h f) -> p h f", h=2),
-                )
+            store_rows("v", a, ip, o)
 
         def bt(n, hh):
             t = eps[(n, hh)]
@@ -330,6 +400,16 @@ def tile_qwen2attention_pa_kernel(
                 in_=o[:].rearrange("p (i f) -> p i f", i=4),
             )
 
+        def tables():
+            zt_ps = psum.tile([P, P], BF16, name="ob0", tag="ob0")
+            nc.tensor.transpose(zt_ps[:], zb[:], ident_b[:])
+            nc.scalar.copy(out=bcol[:], in_=zt_ps[:, 0:24])
+            tb_ps = psum.tile([P, 1024], BF16, name="ob1", tag="ob1")
+            for z in range(2):
+                for i in range(4):
+                    nc.tensor.transpose(tb_ps[:, 512 * z + 128 * i:512 * z + 128 * i + 128], cs_sb[:, i, z, :], ident_b[:])
+            nc.scalar.copy(out=tbT[:], in_=tb_ps[:])
+
         cast(0)
         for g in range(NG):
             tr(0, g)
@@ -345,15 +425,19 @@ def tile_qwen2attention_pa_kernel(
         bcol = const.tile([P, 24], F32, name="bcol")
         tbT = const.tile([P, 1024], BF16, name="tbT")
 
-        for s in range(-1, nu + 1):
+        for s in range(-1, nu + LAG):
             if s in Q_EARLY:
                 qz(s + 1)
             for half in range(2):
                 if 0 <= s < nu:
-                    if UNITS[s][0] == "v":
+                    if UNITS[s][0] == "v" or s in XK:
                         mm_v(s, half)
                     else:
                         mm_ev(s, half)
+                        if s == 0 and half == 0 and TAB_LATE:
+                            tables()
+                        if (s, half) not in V_HEADS:
+                            rope_g(s, half)
                 if s + 3 < nu:
                     cast(s + 3, (half,))
                 for g in (2 * half, 2 * half + 1):
@@ -363,19 +447,13 @@ def tile_qwen2attention_pa_kernel(
                         tr(s + 2, g)
                 if half == 0 and (s, 0) in V_HEADS:
                     rope_v(s, 0)
-                if s >= 1 and UNITS[s - 1][0] != "v":
-                    bt(s - 1, half)
+                b = s - LAG
+                if 0 <= b < nu and UNITS[b][0] != "v" and b not in XK:
+                    bt(b, half)
                     if half == 0:
-                        fin(s - 1, 0)
-            if s == -1:
-                zt_ps = psum.tile([P, P], BF16, name="ob0", tag="ob0")
-                nc.tensor.transpose(zt_ps[:], zb[:], ident_b[:])
-                nc.scalar.copy(out=bcol[:], in_=zt_ps[:, 0:24])
-                tb_ps = psum.tile([P, 1024], BF16, name="ob1", tag="ob1")
-                for z in range(2):
-                    for i in range(4):
-                        nc.tensor.transpose(tb_ps[:, 512 * z + 128 * i:512 * z + 128 * i + 128], cs_sb[:, i, z, :], ident_b[:])
-                nc.scalar.copy(out=tbT[:], in_=tb_ps[:])
+                        fin(b, 0)
+            if s == -1 and not TAB_LATE:
+                tables()
             if s + 1 < nu and s not in Q_EARLY:
                 qz(s + 1)
             if (s, 1) in V_HEADS:
@@ -387,8 +465,14 @@ def tile_qwen2attention_pa_kernel(
                     quantize(xg[gp], c, sc)
                     xc.append(c)
                     xs.append(sc)
+            if s in XK:
+                rope_x(s, 0)
+                rope_x(s, 1)
+            if s - XLAG in XK:
+                fin_x(s - XLAG, 0)
+                fin_x(s - XLAG, 1)
             if 0 <= s < nu and UNITS[s][0] == "v":
                 fin_v(s, 0)
                 fin_v(s, 1)
-            if s >= 1 and UNITS[s - 1][0] != "v":
-                fin(s - 1, 1)
+            if 0 <= b < nu and UNITS[b][0] != "v" and b not in XK:
+                fin(b, 1)

@@ -26,12 +26,12 @@ UNITS = (
 )
 LOADS = (0, 'scl', 'x', 1, 2, 'small')
 KV_AS_LOADED = (1,)
-Q_ORDERED = ()
+Q_ORDERED = ((4, 0), (5, 0), (6, 0), (7, 0), (8, 0))
 Q_ON_VECTOR = ()
-V_HEADS = ((8, 0), (8, 1), (9, 0), (9, 1))
+V_HEADS = ((7, 1), (8, 0), (8, 1), (9, 0), (9, 1))
 Q_EARLY = (8, 9)
 CS_ONCE = True
-TAB_LATE = True
+Q_LATE = ()
 VCOPY = (1,)
 XLAG = 1
 XK = ()
@@ -139,7 +139,7 @@ def tile_qwen2attention_pa_kernel(
         )
 
         def put_in_order(src_words, tag):
-            wpk = work.tile([P, 1024], F32, name=tag, tag=tag, bufs=4)
+            wpk = work.tile([P, 1024], F32, name=tag, tag=tag, bufs=2 if tag == "wpq" else 4)
             nc.scalar.copy(
                 out=wpk[:].rearrange("p (g u w) -> p g u w", g=4, u=2),
                 in_=src_words.rearrange("p (g w u) -> p g u w", g=4, u=2),
@@ -425,26 +425,34 @@ def tile_qwen2attention_pa_kernel(
         bcol = const.tile([P, 24], F32, name="bcol")
         tbT = const.tile([P, 1024], BF16, name="tbT")
 
+        def mm_half(s, half):
+            if UNITS[s][0] == "v" or s in XK:
+                mm_v(s, half)
+            else:
+                mm_ev(s, half)
+                if s == 0 and half == 0:
+                    tables()
+                if (s, half) not in V_HEADS:
+                    rope_g(s, half)
+
         for s in range(-1, nu + LAG):
+            late = s in Q_LATE
             if s in Q_EARLY:
                 qz(s + 1)
             for half in range(2):
-                if 0 <= s < nu:
-                    if UNITS[s][0] == "v" or s in XK:
-                        mm_v(s, half)
-                    else:
-                        mm_ev(s, half)
-                        if s == 0 and half == 0 and TAB_LATE:
-                            tables()
-                        if (s, half) not in V_HEADS:
-                            rope_g(s, half)
+                if 0 <= s < nu and not late:
+                    mm_half(s, half)
                 if s + 3 < nu:
                     cast(s + 3, (half,))
                 for g in (2 * half, 2 * half + 1):
                     if s + 1 < nu:
                         co(s + 1, g)
+                    if late and g == 0:
+                        qz(s)
                     if s + 2 < nu:
                         tr(s + 2, g)
+                if late:
+                    mm_half(s, half)
                 if half == 0 and (s, 0) in V_HEADS:
                     rope_v(s, 0)
                 b = s - LAG
@@ -452,9 +460,7 @@ def tile_qwen2attention_pa_kernel(
                     bt(b, half)
                     if half == 0:
                         fin(b, 0)
-            if s == -1 and not TAB_LATE:
-                tables()
-            if s + 1 < nu and s not in Q_EARLY:
+            if s + 1 < nu and s not in Q_EARLY and s + 1 not in Q_LATE:
                 qz(s + 1)
             if (s, 1) in V_HEADS:
                 rope_v(s, 1)
@@ -465,14 +471,14 @@ def tile_qwen2attention_pa_kernel(
                     quantize(xg[gp], c, sc)
                     xc.append(c)
                     xs.append(sc)
+            if 0 <= s < nu and UNITS[s][0] == "v":
+                fin_v(s, 0)
+                fin_v(s, 1)
             if s in XK:
                 rope_x(s, 0)
                 rope_x(s, 1)
             if s - XLAG in XK:
                 fin_x(s - XLAG, 0)
                 fin_x(s - XLAG, 1)
-            if 0 <= s < nu and UNITS[s][0] == "v":
-                fin_v(s, 0)
-                fin_v(s, 1)
             if 0 <= b < nu and UNITS[b][0] != "v" and b not in XK:
                 fin(b, 1)

@@ -28,13 +28,25 @@ LOADS = (0, 'scl', 'x', 1, 2, 'small')
 KV_AS_LOADED = (1,)
 Q_ORDERED = ((4, 0), (5, 0), (6, 0), (7, 0), (8, 0))
 Q_ON_VECTOR = ()
-V_HEADS = ((7, 1), (8, 0), (8, 1), (9, 0), (9, 1))
+V_HEADS = ((7, 1), (8, 0), (8, 1))
 Q_EARLY = (8, 9)
 CS_ONCE = True
 Q_LATE = ()
 VCOPY = (1,)
-XLAG = 1
-XK = ()
+SCL_SECOND = True
+SPLIT0 = True
+TAILB = True
+XQ_SPLIT = True
+X_SINGLE = False
+CHUNK2 = True
+FINV = ()
+XLAG = 2
+PRE = 0
+PRE_AT = 1
+PRE_HALF = 1
+VTR = ((10, 3), (11, 3))
+XV = ()
+XK = (9,)
 LAG = 1
 STEP_ALL = True
 CHUNKED = (0,)
@@ -84,6 +96,14 @@ def tile_qwen2attention_pa_kernel(
         zb = const.tile([P, P], BF16, name="zb")
         nc.vector.memset(zb[:], 0.0)
 
+        scl = const.tile([P, 16], F32, name="scl")
+
+        def load_scl():
+            nc.sync.dma_start(
+                out=scl[:].rearrange("p (g t) -> p g t", t=4),
+                in_=Wq_scale.rearrange("o (g p t) -> p (o g) t", p=P, t=4),
+            )
+
         def load_unit(n):
             kind, a = UNITS[n]
             if kind == "q":
@@ -92,10 +112,21 @@ def tile_qwen2attention_pa_kernel(
                 r0 = UW * a + (512 if kind == "v" else 0)
                 dt, src, nm = BF16, Wkv[r0:r0 + UW, :], "wkv_%d" % n
             view = src.rearrange("(t p) k -> p t k", p=P)
+            if n in CHUNKED and CHUNK2:
+                ta = rawp.tile([P, 2, 512], dt, name=nm + "a")
+                nc.sync.dma_start(out=ta[:], in_=view[:, :, 0:512])
+                if SCL_SECOND:
+                    load_scl()
+                tl = rawp.tile([P, 2, E - 512], dt, name=nm + "b")
+                nc.sync.dma_start(out=tl[:], in_=view[:, :, 512:E])
+                raw[n] = (ta, tl)
+                return
             if n in CHUNKED:
                 tl = rawp.tile([P, NG, 2, 512], dt, name=nm)
                 for g in range(NG):
                     nc.sync.dma_start(out=tl[:, g, :, :], in_=view[:, :, 512 * g:512 * g + 512])
+                    if g == 0 and SCL_SECOND:
+                        load_scl()
                 raw[n] = tl
                 return
             tl = rawp.tile([P, 2, E], dt, name=nm)
@@ -103,15 +134,12 @@ def tile_qwen2attention_pa_kernel(
             for t in range(2):
                 raw[(n, t)] = tl[:, t, :]
 
-        scl = const.tile([P, 16], F32, name="scl")
         x_sb = []
         cs_sb = const.tile([P, 4, 2, P], BF16, name="cs_sb")
         for item in LOADS + tuple(n for n in range(nu) if n not in LOADS):
             if item == "scl":
-                nc.sync.dma_start(
-                    out=scl[:].rearrange("p (g t) -> p g t", t=4),
-                    in_=Wq_scale.rearrange("o (g p t) -> p (o g) t", p=P, t=4),
-                )
+                if not SCL_SECOND:
+                    load_scl()
             elif item == "x":
                 for i in range(4):
                     xt = rawp.tile([P, E], BF16, name="x_sb%d" % i)
@@ -125,9 +153,11 @@ def tile_qwen2attention_pa_kernel(
                 nc.sync.dma_start(out=zb[16:24, :], in_=bkv.rearrange("(h f) -> h f", f=P))
             else:
                 load_unit(item)
-        if XK:
-            bbk = const.tile([P, 512], BF16, name="bbk")
-            nc.sync.dma_start(out=bbk[:], in_=bkv[0:512].partition_broadcast(P))
+        bbx = {}
+        for n in XK:
+            kind, a = UNITS[n]
+            bbx[n] = const.tile([P, UW], BF16, name="bbx%d" % n)
+            nc.sync.dma_start(out=bbx[n][:], in_=(bq if kind == "q" else bkv)[UW * a:UW * a + UW].partition_broadcast(P))
         bbv = const.tile([P, 512], BF16, name="bbv")
         nc.sync.dma_start(out=bbv[:], in_=bkv[512:1024].partition_broadcast(P))
         if CS_ONCE:
@@ -156,7 +186,18 @@ def tile_qwen2attention_pa_kernel(
                 return
             if n in CHUNKED:
                 wbc = work.tile([P, NG, 2, 512], BF16, name="wbc", tag="wbc", bufs=1)
-                for g in range(NG):
+                for g in range(NG if CHUNK2 else 0):
+                    for t in tiles:
+                        src = raw[n][0][:, t, :] if g == 0 else raw[n][1][:, t, 512 * g - 512:512 * g]
+                        if g == 0 and t == 1 and SPLIT0:
+                            nc.vector.tensor_copy(out=wbc[:, g, t, :], in_=src.bitcast(FP8))
+                        else:
+                            nc.scalar.copy(out=wbc[:, g, t, :], in_=src.bitcast(FP8))
+                for g in range(0 if CHUNK2 else NG):
+                    if g == 0 and SPLIT0:
+                        nc.scalar.copy(out=wbc[:, g, 0, :], in_=raw[n][:, g, 0, :].bitcast(FP8))
+                        nc.vector.tensor_copy(out=wbc[:, g, 1, :], in_=raw[n][:, g, 1, :].bitcast(FP8))
+                        continue
                     nc.scalar.copy(
                         out=wbc[:, g, :, :].rearrange("p t k -> p (t k)"),
                         in_=raw[n][:, g, :, :].rearrange("p t k -> p (t k)").bitcast(FP8),
@@ -241,7 +282,7 @@ def tile_qwen2attention_pa_kernel(
             if UNITS[n][0] != "q" and n not in VCOPY:
                 if g == 0:
                     grp[n] = new_grp()
-                copy_out_plain(tpt[(n, g)], grp[n], 1024 * g)
+                copy_out_plain(tpt[(n, g)], grp[n], 1024 * g, (n, g) in VTR)
 
         def co(n, g):
             if UNITS[n][0] == "q":
@@ -312,8 +353,13 @@ def tile_qwen2attention_pa_kernel(
 
         def mm_v(n, ip):
             c, s = codes[n]
-            acc = psum.tile([P, 512], F32, name="ac%d" % ip, tag="ac%d" % ip)
+            if not (TAILB and n == nu - 1):
+                acc = psum.tile([P, 512], F32, name="ac%d" % ip, tag="ac%d" % ip)
             for il in range(2):
+                if TAILB and n == nu - 1:
+                    b1 = "tp%d" % (2 * ip + il)
+                    acc = psum.tile([P, 512], F32, name=b1, tag=b1)
+                    accs[(n, ip, il)] = acc
                 for g in range(NG):
                     x0 = 512 * (g % 2) + 128 * (2 * ip + il)
                     wcol = slice(256 * g, 256 * g + 256)
@@ -334,12 +380,12 @@ def tile_qwen2attention_pa_kernel(
             nc.vector.tensor_tensor(
                 out=av[:].rearrange("p (i f) -> p i f", i=2),
                 in0=accs[(n, ip)][:].rearrange("p (i f) -> p i f", i=2),
-                in1=bbk[:, UW * a:UW * a + UW].rearrange("p (o f) -> p o f", o=1).to_broadcast([P, 2, UW]),
+                in1=bbx[n][:].rearrange("p (o f) -> p o f", o=1).to_broadcast([P, 2, UW]),
                 op=ADD,
             )
             t12 = work.tile([P, 1024], F32, name="t12", tag="t12", bufs=2 + 2 * LAG)
             for il in range(2):
-                nc.gpsimd.tensor_tensor(
+                (nc.vector if (n, ip) in XV else nc.gpsimd).tensor_tensor(
                     out=t12[:, 512 * il:512 * il + 512].rearrange("p (z h f) -> p z h f", z=2, h=2),
                     in0=av[:, 256 * il:256 * il + 256].rearrange("p (o h f) -> p o h f", o=1, h=2).to_broadcast([P, 2, 2, P]),
                     in1=cs_sb[:, 2 * ip + il, :, :].rearrange("p z (o f) -> p z o f", o=1).to_broadcast([P, 2, 2, P]),
@@ -358,10 +404,10 @@ def tile_qwen2attention_pa_kernel(
                     in1=t[:, il, 1, :, ::-1, :],
                     op=ADD,
                 )
-            store_rows("k", a, ip, o)
+            store_rows(UNITS[n][0], a, ip, o)
 
-        def store_rows(kind, a, ip, o):
-            for il in range(2):
+        def store_rows(kind, a, ip, o, ils=(0, 1)):
+            for il in ils:
                 i = 2 * ip + il
                 nc.sync.dma_start(
                     out=outs[kind][2 * a:2 * a + 2, 128 * i:128 * i + 128, :].rearrange("h p f -> p h f"),
@@ -371,6 +417,12 @@ def tile_qwen2attention_pa_kernel(
         def fin_v(n, ip):
             a = UNITS[n][1]
             o = work.tile([P, 512], F32, name="o", tag="o", bufs=4)
+            if TAILB and n == nu - 1:
+                for il in range(2):
+                    col = slice(UW * il, UW * il + UW)
+                    nc.vector.tensor_tensor(out=o[:, col], in0=accs[(n, ip, il)][:, col], in1=bbv[:, UW * a:UW * a + UW], op=ADD)
+                    store_rows("v", a, ip, o, (il,))
+                return
             nc.vector.tensor_tensor(
                 out=o[:].rearrange("p (i f) -> p i f", i=2),
                 in0=accs[(n, ip)][:].rearrange("p (i f) -> p i f", i=2),
@@ -394,7 +446,10 @@ def tile_qwen2attention_pa_kernel(
         def fin(n, hh):
             kind, a = UNITS[n]
             o = work.tile([P, 512], F32, name="o", tag="o", bufs=4)
-            nc.scalar.copy(out=o[:], in_=obs[(n, hh)][:])
+            if (n, hh) in FINV:
+                nc.vector.tensor_copy(out=o[:], in_=obs[(n, hh)][:])
+            else:
+                nc.scalar.copy(out=o[:], in_=obs[(n, hh)][:])
             nc.sync.dma_start(
                 out=outs[kind][2 * a + hh, :, :].rearrange("(i p) f -> p i f", p=P),
                 in_=o[:].rearrange("p (i f) -> p i f", i=4),
@@ -417,7 +472,21 @@ def tile_qwen2attention_pa_kernel(
         xs = []
         xg = [new_grp(), new_grp()]
         xbanks = ("ac0", "ac1", "ob0", "ob1")
-        for ip in range(2):
+        if X_SINGLE:
+            for i in range(4):
+                xw = x_sb[i][:].bitcast(F32)
+                for j in range(2):
+                    b1 = xbanks[(2 * i + j) % 4]
+                    tp = psum.tile([P, 512], F32, name=b1, tag=b1)
+                    for pp in range(2):
+                        for u in range(2):
+                            c0 = 256 * (2 * j + pp)
+                            nc.tensor.transpose(tp[:, 256 * pp + u:256 * pp + 256:2], xw[:, c0 + u:c0 + 256:2], ident_f[:])
+                    nc.scalar.copy(
+                        out=xg[j][:].bitcast(F32).rearrange("p (q c) -> p q c", q=2)[:, :, 256 * i:256 * i + 256],
+                        in_=tp[:].rearrange("p (q c) -> p q c", q=2),
+                    )
+        for ip in range(0 if X_SINGLE else 2):
             for g in range(NG):
                 tp = transpose_bank(((x_sb[2 * ip][:].bitcast(F32), False), (x_sb[2 * ip + 1][:].bitcast(F32), False)), g, xbanks[g])
                 copy_out_plain(tp, xg[g // 2], 2048 * (g % 2) + 1024 * ip)
@@ -435,6 +504,7 @@ def tile_qwen2attention_pa_kernel(
                 if (s, half) not in V_HEADS:
                     rope_g(s, half)
 
+        pre = [(n, t) for n in range(nu) if UNITS[n][0] != "q" and n not in KV_AS_LOADED for t in range(2)]
         for s in range(-1, nu + LAG):
             late = s in Q_LATE
             if s in Q_EARLY:
@@ -442,8 +512,10 @@ def tile_qwen2attention_pa_kernel(
             for half in range(2):
                 if 0 <= s < nu and not late:
                     mm_half(s, half)
-                if s + 3 < nu:
+                if s + 3 < nu and (UNITS[s + 3][0] == "q" or s + 3 in KV_AS_LOADED or not PRE):
                     cast(s + 3, (half,))
+                if half == PRE_HALF and PRE and 0 <= s - PRE_AT < len(pre):
+                    cast(pre[s - PRE_AT][0], (pre[s - PRE_AT][1],))
                 for g in (2 * half, 2 * half + 1):
                     if s + 1 < nu:
                         co(s + 1, g)
@@ -455,6 +527,8 @@ def tile_qwen2attention_pa_kernel(
                     mm_half(s, half)
                 if half == 0 and (s, 0) in V_HEADS:
                     rope_v(s, 0)
+                if s in XK:
+                    rope_x(s, half)
                 b = s - LAG
                 if 0 <= b < nu and UNITS[b][0] != "v" and b not in XK:
                     bt(b, half)
@@ -468,15 +542,21 @@ def tile_qwen2attention_pa_kernel(
                 for gp in range(2):
                     c = const.tile([P, 1024], U32, name="xc%d" % gp, align_bytes=64)
                     sc = const.tile([P, 1024], U8, name="xs%d" % gp, align_bytes=64)
-                    quantize(xg[gp], c, sc)
+                    if not XQ_SPLIT:
+                        quantize(xg[gp], c, sc)
                     xc.append(c)
                     xs.append(sc)
+                for ip in range(2 if XQ_SPLIT else 0):
+                    for g in range(NG):
+                        c0 = 512 * (g % 2) + 256 * ip
+                        nc.vector.quantize_mx(
+                            out=xc[g // 2][:, c0:c0 + 256].bitcast(FP8X4),
+                            scales=xs[g // 2][:, c0:c0 + 256],
+                            in_=xg[g // 2][:, 4 * c0:4 * c0 + 1024],
+                        )
             if 0 <= s < nu and UNITS[s][0] == "v":
                 fin_v(s, 0)
                 fin_v(s, 1)
-            if s in XK:
-                rope_x(s, 0)
-                rope_x(s, 1)
             if s - XLAG in XK:
                 fin_x(s - XLAG, 0)
                 fin_x(s - XLAG, 1)

@@ -28,7 +28,7 @@ LOADS = (0, 'scl', 'x', 1, 2, 'small')
 KV_AS_LOADED = (1,)
 Q_ORDERED = ((4, 0), (5, 0), (6, 0), (7, 0), (8, 0))
 Q_ON_VECTOR = ()
-V_HEADS = ((7, 1), (8, 0), (8, 1))
+V_HEADS = ((7, 1), (9, 0), (9, 1))
 Q_EARLY = (8, 9)
 CS_ONCE = True
 Q_LATE = ()
@@ -39,14 +39,24 @@ TAILB = True
 XQ_SPLIT = True
 X_SINGLE = False
 CHUNK2 = True
-FINV = ()
-XLAG = 2
+FINV = ((7, 0),)
+GPAIR = ()
+LAG2 = ()
+AV2 = 2
+T22 = 3
+V_WIDE = ()
+HEADK = 0
+Q1_LAST = True
+QX = True
+OB = 6
+XPRE = (False, False)
+XLAG = (1, 1)
 PRE = 0
 PRE_AT = 1
 PRE_HALF = 1
-VTR = ((10, 3), (11, 3))
-XV = ()
-XK = (9,)
+VTR = ()
+XV = ((8, 0), (8, 1))
+XK = (8,)
 LAG = 1
 STEP_ALL = True
 CHUNKED = (0,)
@@ -218,7 +228,10 @@ def tile_qwen2attention_pa_kernel(
                     words[(n, t)] = (wbs[t][:].bitcast(F32), "ugp")
                 return
             for t in tiles:
-                nc.scalar.copy(out=wbs[t][:], in_=raw[(n, t)].bitcast(FP8))
+                if (n, t) in V_WIDE:
+                    nc.vector.tensor_copy(out=wbs[t][:], in_=raw[(n, t)].bitcast(FP8))
+                else:
+                    nc.scalar.copy(out=wbs[t][:], in_=raw[(n, t)].bitcast(FP8))
             for t in tiles:
                 if (n, t) in Q_ORDERED:
                     words[(n, t)] = (put_in_order(wbs[t][:].bitcast(F32), "wpq"), True)
@@ -337,7 +350,28 @@ def tile_qwen2attention_pa_kernel(
                     op0=ADD, op1=MULT,
                 )
 
+        avs = {}
+
         def rope_g(n, hh):
+            if n not in GPAIR:
+                rope_g1(n, hh)
+                return
+            if hh == 0:
+                avs[n] = work.tile([P, 1024], F32, name="av2", tag="av2", bufs=AV2)
+            h = head_of(n, hh)
+            nc.scalar.activation(out=avs[n][:, 512 * hh:512 * hh + 512], in_=accs[(n, hh)][:], func=IDENT, bias=bcol[:, h:h + 1], scale=1.0)
+            if hh == 1:
+                t2 = work.tile([P, 2048], F32, name="t22", tag="t22", bufs=T22)
+                nc.gpsimd.tensor_tensor(
+                    out=t2[:].rearrange("p (h z c) -> p h z c", h=2, z=2),
+                    in0=avs[n][:].rearrange("p (h o c) -> p h o c", h=2, o=1).to_broadcast([P, 2, 2, 512]),
+                    in1=tbT[:].rearrange("p (o z c) -> p o z c", o=1, z=2).to_broadcast([P, 2, 2, 512]),
+                    op=MULT,
+                )
+                for k in range(2):
+                    eps[(n, k)] = t2[:, 1024 * k:1024 * k + 1024]
+
+        def rope_g1(n, hh):
             acc = accs[(n, hh)]
             h = head_of(n, hh)
             t12 = work.tile([P, 1024], F32, name="t12", tag="t12", bufs=2 + 2 * LAG)
@@ -396,7 +430,7 @@ def tile_qwen2attention_pa_kernel(
         def fin_x(n, ip):
             a = UNITS[n][1]
             t = eps[(n, ip)][:].rearrange("p (i z h w f) -> p i z h w f", i=2, z=2, h=2, w=2)
-            o = work.tile([P, 512], F32, name="o", tag="o", bufs=4)
+            o = work.tile([P, 512], F32, name="o", tag="o", bufs=OB)
             for il in range(2):
                 nc.vector.tensor_tensor(
                     out=o[:, 256 * il:256 * il + 256].rearrange("p (h w f) -> p h w f", h=2, w=2),
@@ -416,7 +450,7 @@ def tile_qwen2attention_pa_kernel(
 
         def fin_v(n, ip):
             a = UNITS[n][1]
-            o = work.tile([P, 512], F32, name="o", tag="o", bufs=4)
+            o = work.tile([P, 512], F32, name="o", tag="o", bufs=OB)
             if TAILB and n == nu - 1:
                 for il in range(2):
                     col = slice(UW * il, UW * il + UW)
@@ -432,7 +466,7 @@ def tile_qwen2attention_pa_kernel(
             store_rows("v", a, ip, o)
 
         def bt(n, hh):
-            t = eps[(n, hh)]
+            t = eps[(n, hh)] if n in GPAIR else eps[(n, hh)][:]
             ob = psum.tile([P, 512], F32, name="ob%d" % hh, tag="ob%d" % hh)
             for i in range(4):
                 col = slice(128 * i, 128 * i + 128)
@@ -445,7 +479,7 @@ def tile_qwen2attention_pa_kernel(
 
         def fin(n, hh):
             kind, a = UNITS[n]
-            o = work.tile([P, 512], F32, name="o", tag="o", bufs=4)
+            o = work.tile([P, 512], F32, name="o", tag="o", bufs=OB)
             if (n, hh) in FINV:
                 nc.vector.tensor_copy(out=o[:], in_=obs[(n, hh)][:])
             else:
@@ -468,6 +502,12 @@ def tile_qwen2attention_pa_kernel(
         cast(0)
         for g in range(NG):
             tr(0, g)
+        if HEADK:
+            cast(1)
+            for g in range(NG):
+                co(0, g)
+                tr(1, g)
+            qz(0)
         xc = []
         xs = []
         xg = [new_grp(), new_grp()]
@@ -490,7 +530,8 @@ def tile_qwen2attention_pa_kernel(
             for g in range(NG):
                 tp = transpose_bank(((x_sb[2 * ip][:].bitcast(F32), False), (x_sb[2 * ip + 1][:].bitcast(F32), False)), g, xbanks[g])
                 copy_out_plain(tp, xg[g // 2], 2048 * (g % 2) + 1024 * ip)
-        cast(1)
+        if not HEADK:
+            cast(1)
         bcol = const.tile([P, 24], F32, name="bcol")
         tbT = const.tile([P, 1024], BF16, name="tbT")
 
@@ -505,39 +546,49 @@ def tile_qwen2attention_pa_kernel(
                     rope_g(s, half)
 
         pre = [(n, t) for n in range(nu) if UNITS[n][0] != "q" and n not in KV_AS_LOADED for t in range(2)]
-        for s in range(-1, nu + LAG):
+        back = {}
+        for n in range(nu):
+            if UNITS[n][0] != "v" and n not in XK:
+                back.setdefault(n + (2 if n in LAG2 else 1), []).append(n)
+        for s in range(-1, nu + 2):
             late = s in Q_LATE
-            if s in Q_EARLY:
+            if s in Q_EARLY and (s not in XK or not QX):
                 qz(s + 1)
             for half in range(2):
                 if 0 <= s < nu and not late:
                     mm_half(s, half)
+                if s in XK:
+                    rope_x(s, half)
+                    if half == 0 and QX:
+                        qz(s + 1)
                 if s + 3 < nu and (UNITS[s + 3][0] == "q" or s + 3 in KV_AS_LOADED or not PRE):
                     cast(s + 3, (half,))
                 if half == PRE_HALF and PRE and 0 <= s - PRE_AT < len(pre):
                     cast(pre[s - PRE_AT][0], (pre[s - PRE_AT][1],))
                 for g in (2 * half, 2 * half + 1):
-                    if s + 1 < nu:
+                    if s + 1 < nu and not (HEADK and s == -1) and not (HEADK == 3 and s == 0):
                         co(s + 1, g)
                     if late and g == 0:
                         qz(s)
-                    if s + 2 < nu:
+                    if s + 2 < nu and not (HEADK and s == -1):
                         tr(s + 2, g)
                 if late:
                     mm_half(s, half)
                 if half == 0 and (s, 0) in V_HEADS:
                     rope_v(s, 0)
-                if s in XK:
-                    rope_x(s, half)
-                b = s - LAG
-                if 0 <= b < nu and UNITS[b][0] != "v" and b not in XK:
+                for b in back.get(s, ()):
                     bt(b, half)
                     if half == 0:
                         fin(b, 0)
-            if s + 1 < nu and s not in Q_EARLY and s + 1 not in Q_LATE:
+            if s + 1 < nu and s not in Q_EARLY and s + 1 not in Q_LATE and not (HEADK and s == -1) and not (HEADK == 3 and s == 0):
                 qz(s + 1)
             if (s, 1) in V_HEADS:
                 rope_v(s, 1)
+            if s == -1 and HEADK == 3:
+                for g in range(NG):
+                    co(1, g)
+                if not Q1_LAST:
+                    qz(1)
             if s == -1:
                 for gp in range(2):
                     c = const.tile([P, 1024], U32, name="xc%d" % gp, align_bytes=64)
@@ -554,11 +605,16 @@ def tile_qwen2attention_pa_kernel(
                             scales=xs[g // 2][:, c0:c0 + 256],
                             in_=xg[g // 2][:, 4 * c0:4 * c0 + 1024],
                         )
+                if HEADK == 3 and Q1_LAST:
+                    qz(1)
+            for ip in range(2):
+                if s - XLAG[ip] in XK and XPRE[ip]:
+                    fin_x(s - XLAG[ip], ip)
             if 0 <= s < nu and UNITS[s][0] == "v":
                 fin_v(s, 0)
                 fin_v(s, 1)
-            if s - XLAG in XK:
-                fin_x(s - XLAG, 0)
-                fin_x(s - XLAG, 1)
-            if 0 <= b < nu and UNITS[b][0] != "v" and b not in XK:
+            for ip in range(2):
+                if s - XLAG[ip] in XK and not XPRE[ip]:
+                    fin_x(s - XLAG[ip], ip)
+            for b in back.get(s, ()):
                 fin(b, 1)

@@ -33,7 +33,7 @@ Q_EARLY = (8, 9)
 CS_ONCE = True
 Q_LATE = ()
 VCOPY = (1,)
-SCL_SECOND = True
+SCL_SECOND = False
 SPLIT0 = True
 TAILB = True
 XQ_SPLIT = True
@@ -44,6 +44,9 @@ GPAIR = ()
 LAG2 = ()
 AV2 = 2
 T22 = 3
+KSPLIT = (1,)
+TBL = {}
+MERGE = ()
 V_WIDE = ()
 HEADK = 0
 Q1_LAST = True
@@ -129,6 +132,8 @@ def tile_qwen2attention_pa_kernel(
                     load_scl()
                 tl = rawp.tile([P, 2, E - 512], dt, name=nm + "b")
                 nc.sync.dma_start(out=tl[:], in_=view[:, :, 512:E])
+                if not SCL_SECOND:
+                    load_scl()
                 raw[n] = (ta, tl)
                 return
             if n in CHUNKED:
@@ -140,7 +145,11 @@ def tile_qwen2attention_pa_kernel(
                 raw[n] = tl
                 return
             tl = rawp.tile([P, 2, E], dt, name=nm)
-            nc.sync.dma_start(out=tl[:], in_=view)
+            if n in KSPLIT:
+                for t in range(2):
+                    nc.sync.dma_start(out=tl[:, t, :], in_=view[:, t, :])
+            else:
+                nc.sync.dma_start(out=tl[:], in_=view)
             for t in range(2):
                 raw[(n, t)] = tl[:, t, :]
 
@@ -148,17 +157,16 @@ def tile_qwen2attention_pa_kernel(
         cs_sb = const.tile([P, 4, 2, P], BF16, name="cs_sb")
         for item in LOADS + tuple(n for n in range(nu) if n not in LOADS):
             if item == "scl":
-                if not SCL_SECOND:
-                    load_scl()
+                pass
             elif item == "x":
                 for i in range(4):
                     xt = rawp.tile([P, E], BF16, name="x_sb%d" % i)
-                    nc.sync.dma_start(out=xt[:], in_=xf[128 * i:128 * i + 128, :])
+                    nc.sync.dma_start(out=xt[:], in_=xf.rearrange("(p i) k -> p i k", i=4)[:, i, :])
                     x_sb.append(xt)
             elif item == "small":
                 for w in range(1 if CS_ONCE else 2):
-                    nc.sync.dma_start(out=cs_sb[:, :, 0, 64 * w:64 * w + 64], in_=cos.rearrange("(i p) j -> p i j", p=P))
-                    nc.sync.dma_start(out=cs_sb[:, :, 1, 64 * w:64 * w + 64], in_=sin.rearrange("(i p) j -> p i j", p=P))
+                    nc.sync.dma_start(out=cs_sb[:, :, 0, 64 * w:64 * w + 64], in_=cos.rearrange("(p i) j -> p i j", p=P))
+                    nc.sync.dma_start(out=cs_sb[:, :, 1, 64 * w:64 * w + 64], in_=sin.rearrange("(p i) j -> p i j", p=P))
                 nc.sync.dma_start(out=zb[0:16, :], in_=bq.rearrange("(h f) -> h f", f=P))
                 nc.sync.dma_start(out=zb[16:24, :], in_=bkv.rearrange("(h f) -> h f", f=P))
             else:
@@ -238,9 +246,13 @@ def tile_qwen2attention_pa_kernel(
                 else:
                     words[(n, t)] = (wbs[t][:].bitcast(F32), False)
 
+        def transpose_tile(w2, t, g, tp):
+            for u in range(2):
+                nc.tensor.transpose(tp[:, 256 * t + u:256 * t + 256:2], w2[t][0][:, 256 * g + u:256 * (g + 1):2], ident_f[:])
+
         def transpose_bank(w2, g, bank):
             tp = psum.tile([P, 512], F32, name=bank, tag=bank)
-            stepped = STEP_ALL or w2[0][1] in (False, "chunks")
+            stepped = w2[0][1] is not True or w2[1][1] is not True
             for t in range(2):
                 w, ordered = w2[t]
                 for u in range(2):
@@ -291,6 +303,14 @@ def tile_qwen2attention_pa_kernel(
             )
 
         def tr(n, g):
+            if n in KSPLIT:
+                if g == NG - 1:
+                    for k in range(NG):
+                        tpt[(n, k)] = (psum.tile([P, 512], F32, name="tp%d" % k, tag="tp%d" % k), True)
+                    for t in range(2):
+                        for k in range(NG):
+                            transpose_tile((words[(n, 0)], words[(n, 1)]), t, k, tpt[(n, k)][0])
+                return
             tpt[(n, g)] = transpose_bank((words[(n, 0)], words[(n, 1)]), g, "tp%d" % g)
             if UNITS[n][0] != "q" and n not in VCOPY:
                 if g == 0:
@@ -417,6 +437,14 @@ def tile_qwen2attention_pa_kernel(
                 in1=bbx[n][:].rearrange("p (o f) -> p o f", o=1).to_broadcast([P, 2, UW]),
                 op=ADD,
             )
+            avx[(n, ip)] = av
+            if not TBL:
+                prod_x(n, ip)
+
+        avx = {}
+
+        def prod_x(n, ip):
+            av = avx[(n, ip)]
             t12 = work.tile([P, 1024], F32, name="t12", tag="t12", bufs=2 + 2 * LAG)
             for il in range(2):
                 (nc.vector if (n, ip) in XV else nc.gpsimd).tensor_tensor(
@@ -433,7 +461,7 @@ def tile_qwen2attention_pa_kernel(
             o = work.tile([P, 512], F32, name="o", tag="o", bufs=OB)
             for il in range(2):
                 nc.vector.tensor_tensor(
-                    out=o[:, 256 * il:256 * il + 256].rearrange("p (h w f) -> p h w f", h=2, w=2),
+                    out=o[:].rearrange("p (h i w f) -> p i h w f", h=2, i=2, w=2)[:, il, :, :, :],
                     in0=t[:, il, 0, :, :, :],
                     in1=t[:, il, 1, :, ::-1, :],
                     op=ADD,
@@ -441,11 +469,17 @@ def tile_qwen2attention_pa_kernel(
             store_rows(UNITS[n][0], a, ip, o)
 
         def store_rows(kind, a, ip, o, ils=(0, 1)):
-            for il in ils:
-                i = 2 * ip + il
+            dst = outs[kind][2 * a:2 * a + 2, :, :]
+            if len(ils) == 2:
                 nc.sync.dma_start(
-                    out=outs[kind][2 * a:2 * a + 2, 128 * i:128 * i + 128, :].rearrange("h p f -> p h f"),
-                    in_=o[:, 256 * il:256 * il + 256].rearrange("p (h f) -> p h f", h=2),
+                    out=dst.rearrange("h (p q i) f -> q p h (i f)", q=2, i=2)[ip],
+                    in_=o[:].rearrange("p (h c) -> p h c", h=2),
+                )
+                return
+            for il in ils:
+                nc.sync.dma_start(
+                    out=dst.rearrange("h (p q i) f -> q i p h f", q=2, i=2)[ip, il],
+                    in_=o[:].rearrange("p (h i f) -> p h i f", h=2, i=2)[:, :, il, :],
                 )
 
         def fin_v(n, ip):
@@ -454,13 +488,18 @@ def tile_qwen2attention_pa_kernel(
             if TAILB and n == nu - 1:
                 for il in range(2):
                     col = slice(UW * il, UW * il + UW)
-                    nc.vector.tensor_tensor(out=o[:, col], in0=accs[(n, ip, il)][:, col], in1=bbv[:, UW * a:UW * a + UW], op=ADD)
+                    nc.vector.tensor_tensor(
+                        out=o[:].rearrange("p (h i f) -> p h i f", h=2, i=2)[:, :, il, :],
+                        in0=accs[(n, ip, il)][:, col].rearrange("p (h f) -> p h f", h=2),
+                        in1=bbv[:, UW * a:UW * a + UW].rearrange("p (h f) -> p h f", h=2),
+                        op=ADD,
+                    )
                     store_rows("v", a, ip, o, (il,))
                 return
             nc.vector.tensor_tensor(
-                out=o[:].rearrange("p (i f) -> p i f", i=2),
-                in0=accs[(n, ip)][:].rearrange("p (i f) -> p i f", i=2),
-                in1=bbv[:, UW * a:UW * a + UW].rearrange("p (o f) -> p o f", o=1).to_broadcast([P, 2, UW]),
+                out=o[:].rearrange("p (h i f) -> p i h f", h=2, i=2),
+                in0=accs[(n, ip)][:].rearrange("p (i h f) -> p i h f", i=2, h=2),
+                in1=bbv[:, UW * a:UW * a + UW].rearrange("p (o h f) -> p o h f", o=1, h=2).to_broadcast([P, 2, 2, P]),
                 op=ADD,
             )
             store_rows("v", a, ip, o)
@@ -485,8 +524,8 @@ def tile_qwen2attention_pa_kernel(
             else:
                 nc.scalar.copy(out=o[:], in_=obs[(n, hh)][:])
             nc.sync.dma_start(
-                out=outs[kind][2 * a + hh, :, :].rearrange("(i p) f -> p i f", p=P),
-                in_=o[:].rearrange("p (i f) -> p i f", i=4),
+                out=outs[kind][2 * a + hh, :, :].rearrange("(p i) f -> p (i f)", i=4),
+                in_=o[:],
             )
 
         def tables():
@@ -550,13 +589,16 @@ def tile_qwen2attention_pa_kernel(
         for n in range(nu):
             if UNITS[n][0] != "v" and n not in XK:
                 back.setdefault(n + (2 if n in LAG2 else 1), []).append(n)
-        for s in range(-1, nu + 2):
+        for s in range(-1, 8 if TBL else nu + 2):
             late = s in Q_LATE
             if s in Q_EARLY and (s not in XK or not QX):
                 qz(s + 1)
             for half in range(2):
-                if 0 <= s < nu and not late:
+                if 0 <= s < nu and not late and s not in MERGE:
                     mm_half(s, half)
+                if s in MERGE and half == 0:
+                    mm_half(s, 0)
+                    mm_half(s, 1)
                 if s in XK:
                     rope_x(s, half)
                     if half == 0 and QX:
@@ -618,3 +660,39 @@ def tile_qwen2attention_pa_kernel(
                     fin_x(s - XLAG[ip], ip)
             for b in back.get(s, ()):
                 fin(b, 1)
+        def act(item):
+            k = item[0]
+            if k == "q":
+                qz(item[1])
+            elif k == "bias":
+                rope_x(item[1], item[2])
+            elif k == "prod":
+                prod_x(item[1], item[2])
+            elif k == "add":
+                fin_x(item[1], item[2])
+            elif k == "finv":
+                fin_v(item[1], item[2])
+            elif k == "stt":
+                rope_v(item[1], item[2])
+            elif k == "fin":
+                fin(item[1], item[2])
+
+        for s in range(8, nu + 1) if TBL else ():
+            def slot(j):
+                for it in TBL.get((s, j), ()):
+                    act(it)
+            slot(0)
+            for half in range(2):
+                if s < nu:
+                    mm_half(s, half)
+                slot(4 * half + 1)
+                if s + 3 < nu:
+                    cast(s + 3, (half,))
+                for g in (2 * half, 2 * half + 1):
+                    if s + 2 < nu:
+                        tr(s + 2, g)
+                slot(4 * half + 2)
+                for b in back.get(s, ()):
+                    bt(b, half)
+                slot(4 * half + 3)
+            slot(8)

@@ -16,61 +16,26 @@ ADD = mybir.AluOpType.add
 IDENT = mybir.ActivationFunctionType.Identity
 
 P = 128
+HALF = P // 2
 E = 2048
 NG = 4
 UW = 256
+NT = 4
+BANK = 512
 
 UNITS = (
     ("q", 0), ("k", 0), ("q", 1), ("q", 2), ("q", 3), ("q", 4),
     ("q", 5), ("q", 6), ("q", 7), ("k", 1), ("v", 0), ("v", 1),
 )
-LOADS = (0, 'scl', 'x', 1, 2, 'small')
-KV_AS_LOADED = (1,)
-Q_ORDERED = ((4, 0), (5, 0), (6, 0), (7, 0), (8, 0))
-Q_ON_VECTOR = ()
-V_HEADS = ((7, 1), (9, 0), (9, 1))
-Q_EARLY = (8, 9)
-CS_ONCE = True
-Q_LATE = ()
-VCOPY = (1,)
-SCL_SECOND = False
-SPLIT0 = True
-TAILB = True
-XQ_SPLIT = True
-X_SINGLE = False
-CHUNK2 = True
-FINV = ((7, 0),)
-GPAIR = ()
-LAG2 = ()
-AV2 = 2
-T22 = 3
-KSPLIT = (1,)
-TBL = {}
-MERGE = ()
-V_WIDE = ()
-HEADK = 0
-Q1_LAST = True
-QX = True
-OB = 6
-XPRE = (False, False)
-XLAG = (1, 1)
-PRE = 0
-PRE_AT = 1
-PRE_HALF = 1
-VTR = ()
-XV = ((8, 0), (8, 1))
-XK = (8,)
-LAG = 1
-STEP_ALL = True
-CHUNKED = (0,)
+NU = len(UNITS)
+FIRST_Q, FIRST_K, LAST_Q, LAST_K, FIRST_V, LAST_V = 0, 1, 8, 9, 10, 11
+FIRST_ORDERED = 4
 
 
 def tile_qwen2attention_pa_kernel(
     tc, x, Wq_bytes, Wq_scale, bq, Wkv, bkv, cos, sin, out_0, out_1, out_2
 ):
     nc = tc.nc
-    nu = len(UNITS)
-    xf = x.rearrange("b s k -> (b s) k")
     outs = {
         "q": out_0.rearrange("b h s f -> (b h) s f"),
         "k": out_1.rearrange("b h s f -> (b h) s f"),
@@ -79,620 +44,444 @@ def tile_qwen2attention_pa_kernel(
 
     with ExitStack() as ctx:
         const = ctx.enter_context(tc.tile_pool(name="const", bufs=1))
-        rawp = ctx.enter_context(tc.tile_pool(name="raw", bufs=1))
+        loaded = ctx.enter_context(tc.tile_pool(name="loaded", bufs=1))
         work = ctx.enter_context(tc.tile_pool(name="work", bufs=2))
         psum = ctx.enter_context(tc.psum_pool(name="psum", bufs=1))
         ctx.enter_context(tc.manual_schedule())
 
-        raw = {}
-        words = {}
-        tpt = {}
-        grp = {}
-        codes = {}
-        accs = {}
-        eps = {}
-        obs = {}
+        def bank(tag):
+            return psum.tile([P, BANK], F32, name=tag, tag=tag)
 
         ident_f = const.tile([P, P], F32, name="ident_f")
         make_identity(nc, ident_f[:])
         ident_b = const.tile([P, P], BF16, name="ident_b")
         make_identity(nc, ident_b[:])
         swap_f = const.tile([P, P], F32, name="swap_f")
-        nc.gpsimd.tensor_copy(out=swap_f[:, 0:64], in_=ident_f[:, 64:128])
-        nc.gpsimd.tensor_copy(out=swap_f[:, 64:128], in_=ident_f[:, 0:64])
+        nc.gpsimd.tensor_copy(out=swap_f[:, 0:HALF], in_=ident_f[:, HALF:P])
+        nc.gpsimd.tensor_copy(out=swap_f[:, HALF:P], in_=ident_f[:, 0:HALF])
 
         warm = const.tile([P, 2], F32, name="warm")
         nc.vector.memset(warm[:, 0:1], 0.0)
         nc.scalar.copy(out=warm[:, 1:2], in_=warm[:, 0:1])
-        ones = const.tile([P, 1], F32, name="ones")
-        nc.vector.memset(ones[:], 1.0)
-        zb = const.tile([P, P], BF16, name="zb")
-        nc.vector.memset(zb[:], 0.0)
+        bias_rows = const.tile([P, P], BF16, name="bias_rows")
+        nc.vector.memset(bias_rows[:], 0.0)
 
-        scl = const.tile([P, 16], F32, name="scl")
+        wq_first = {}
+        weights = {}
+        x_sb = []
+        scales = const.tile([P, NG * 4], F32, name="scales")
+        cs = const.tile([P, NT, 2, P], BF16, name="cs")
 
-        def load_scl():
-            nc.sync.dma_start(
-                out=scl[:].rearrange("p (g t) -> p g t", t=4),
-                in_=Wq_scale.rearrange("o (g p t) -> p (o g) t", p=P, t=4),
-            )
-
-        def load_unit(n):
+        def rows_of(n):
             kind, a = UNITS[n]
             if kind == "q":
-                dt, src, nm = U8, Wq_bytes[UW * a:UW * a + UW, :], "wq8_%d" % n
+                src = Wq_bytes[UW * a:UW * a + UW, :]
             else:
-                r0 = UW * a + (512 if kind == "v" else 0)
-                dt, src, nm = BF16, Wkv[r0:r0 + UW, :], "wkv_%d" % n
-            view = src.rearrange("(t p) k -> p t k", p=P)
-            if n in CHUNKED and CHUNK2:
-                ta = rawp.tile([P, 2, 512], dt, name=nm + "a")
-                nc.sync.dma_start(out=ta[:], in_=view[:, :, 0:512])
-                if SCL_SECOND:
-                    load_scl()
-                tl = rawp.tile([P, 2, E - 512], dt, name=nm + "b")
-                nc.sync.dma_start(out=tl[:], in_=view[:, :, 512:E])
-                if not SCL_SECOND:
-                    load_scl()
-                raw[n] = (ta, tl)
-                return
-            if n in CHUNKED:
-                tl = rawp.tile([P, NG, 2, 512], dt, name=nm)
-                for g in range(NG):
-                    nc.sync.dma_start(out=tl[:, g, :, :], in_=view[:, :, 512 * g:512 * g + 512])
-                    if g == 0 and SCL_SECOND:
-                        load_scl()
-                raw[n] = tl
-                return
-            tl = rawp.tile([P, 2, E], dt, name=nm)
-            if n in KSPLIT:
+                row = UW * a + (512 if kind == "v" else 0)
+                src = Wkv[row:row + UW, :]
+            return src.rearrange("(t p) k -> p t k", p=P)
+
+        def load_unit(n):
+            tile = loaded.tile([P, 2, E], U8 if UNITS[n][0] == "q" else BF16, name="weights%d" % n)
+            if n == FIRST_K:
                 for t in range(2):
-                    nc.sync.dma_start(out=tl[:, t, :], in_=view[:, t, :])
+                    nc.sync.dma_start(out=tile[:, t, :], in_=rows_of(n)[:, t, :])
             else:
-                nc.sync.dma_start(out=tl[:], in_=view)
+                nc.sync.dma_start(out=tile[:], in_=rows_of(n))
             for t in range(2):
-                raw[(n, t)] = tl[:, t, :]
+                weights[(n, t)] = tile[:, t, :]
 
-        x_sb = []
-        cs_sb = const.tile([P, 4, 2, P], BF16, name="cs_sb")
-        for item in LOADS + tuple(n for n in range(nu) if n not in LOADS):
-            if item == "scl":
-                pass
-            elif item == "x":
-                for i in range(4):
-                    xt = rawp.tile([P, E], BF16, name="x_sb%d" % i)
-                    nc.sync.dma_start(out=xt[:], in_=xf.rearrange("(p i) k -> p i k", i=4)[:, i, :])
-                    x_sb.append(xt)
-            elif item == "small":
-                for w in range(1 if CS_ONCE else 2):
-                    nc.sync.dma_start(out=cs_sb[:, :, 0, 64 * w:64 * w + 64], in_=cos.rearrange("(p i) j -> p i j", p=P))
-                    nc.sync.dma_start(out=cs_sb[:, :, 1, 64 * w:64 * w + 64], in_=sin.rearrange("(p i) j -> p i j", p=P))
-                nc.sync.dma_start(out=zb[0:16, :], in_=bq.rearrange("(h f) -> h f", f=P))
-                nc.sync.dma_start(out=zb[16:24, :], in_=bkv.rearrange("(h f) -> h f", f=P))
-            else:
-                load_unit(item)
-        bbx = {}
-        for n in XK:
-            kind, a = UNITS[n]
-            bbx[n] = const.tile([P, UW], BF16, name="bbx%d" % n)
-            nc.sync.dma_start(out=bbx[n][:], in_=(bq if kind == "q" else bkv)[UW * a:UW * a + UW].partition_broadcast(P))
-        bbv = const.tile([P, 512], BF16, name="bbv")
-        nc.sync.dma_start(out=bbv[:], in_=bkv[512:1024].partition_broadcast(P))
-        if CS_ONCE:
-            nc.gpsimd.tensor_scalar(
-                out=cs_sb[:, :, 0, 64:128], in0=cs_sb[:, :, 0, 0:64], scalar1=1.0, scalar2=0.0, op0=MULT, op1=ADD
-            )
-        nc.gpsimd.tensor_scalar(
-            out=cs_sb[:, :, 1, 64:128], in0=cs_sb[:, :, 1, 0:64] if CS_ONCE else cs_sb[:, :, 1, 64:128], scalar1=-1.0, scalar2=0.0, op0=MULT, op1=ADD
+        for part, (k0, k1) in enumerate(((0, 512), (512, E))):
+            tile = loaded.tile([P, 2, k1 - k0], U8, name="weights0_%d" % part)
+            nc.sync.dma_start(out=tile[:], in_=rows_of(FIRST_Q)[:, :, k0:k1])
+            for g in range(k0 // 512, k1 // 512):
+                wq_first[g] = tile[:, :, 512 * g - k0:512 * g - k0 + 512]
+        nc.sync.dma_start(
+            out=scales[:].rearrange("p (g t) -> p g t", t=4),
+            in_=Wq_scale.rearrange("o (g p t) -> p (o g) t", p=P, t=4),
         )
-
-        def put_in_order(src_words, tag):
-            wpk = work.tile([P, 1024], F32, name=tag, tag=tag, bufs=2 if tag == "wpq" else 4)
-            nc.scalar.copy(
-                out=wpk[:].rearrange("p (g u w) -> p g u w", g=4, u=2),
-                in_=src_words.rearrange("p (g w u) -> p g u w", g=4, u=2),
+        x_rows = x.rearrange("b s k -> (b s) k")
+        for i in range(NT):
+            tile = loaded.tile([P, E], BF16, name="x%d" % i)
+            nc.sync.dma_start(out=tile[:], in_=x_rows[P * i:P * i + P, :])
+            x_sb.append(tile)
+        load_unit(1)
+        load_unit(2)
+        nc.sync.dma_start(out=cs[:, :, 0, 0:HALF], in_=cos.rearrange("(i p) j -> p i j", p=P))
+        nc.sync.dma_start(out=cs[:, :, 1, 0:HALF], in_=sin.rearrange("(i p) j -> p i j", p=P))
+        nc.sync.dma_start(out=bias_rows[0:16, :], in_=bq.rearrange("(h f) -> h f", f=P))
+        nc.sync.dma_start(out=bias_rows[16:24, :], in_=bkv.rearrange("(h f) -> h f", f=P))
+        for n in range(3, NU):
+            load_unit(n)
+        bias_q = const.tile([P, UW], BF16, name="bias_q")
+        a = UNITS[LAST_Q][1]
+        nc.sync.dma_start(out=bias_q[:], in_=bq[UW * a:UW * a + UW].partition_broadcast(P))
+        bias_v = const.tile([P, 2 * UW], BF16, name="bias_v")
+        nc.sync.dma_start(out=bias_v[:], in_=bkv[512:1024].partition_broadcast(P))
+        for z, sign in ((0, 1.0), (1, -1.0)):
+            nc.gpsimd.tensor_scalar(
+                out=cs[:, :, z, HALF:P], in0=cs[:, :, z, 0:HALF], scalar1=sign, scalar2=0.0, op0=MULT, op1=ADD
             )
-            return wpk[:]
 
-        def cast(n, tiles=(0, 1)):
+        words = {}
+        turned = {}
+        groups = {}
+        codes = {}
+
+        def order_words(src, tag, bufs):
+            dst = work.tile([P, E // 2], F32, name=tag, tag=tag, bufs=bufs)
+            nc.scalar.copy(
+                out=dst[:].rearrange("p (g u w) -> p g u w", g=NG, u=2),
+                in_=src.rearrange("p (g w u) -> p g u w", g=NG, u=2),
+            )
+            return dst[:]
+
+        def prepare(n, t):
             if UNITS[n][0] != "q":
-                for t in tiles:
-                    if n in KV_AS_LOADED:
-                        words[(n, t)] = (raw[(n, t)].bitcast(F32), False)
-                    else:
-                        words[(n, t)] = (put_in_order(raw[(n, t)].bitcast(F32), "wpk"), True)
+                words[(n, t)] = (order_words(weights[(n, t)].bitcast(F32), "ordered_kv", 4), True)
                 return
-            if n in CHUNKED:
-                wbc = work.tile([P, NG, 2, 512], BF16, name="wbc", tag="wbc", bufs=1)
-                for g in range(NG if CHUNK2 else 0):
-                    for t in tiles:
-                        src = raw[n][0][:, t, :] if g == 0 else raw[n][1][:, t, 512 * g - 512:512 * g]
-                        if g == 0 and t == 1 and SPLIT0:
-                            nc.vector.tensor_copy(out=wbc[:, g, t, :], in_=src.bitcast(FP8))
-                        else:
-                            nc.scalar.copy(out=wbc[:, g, t, :], in_=src.bitcast(FP8))
-                for g in range(0 if CHUNK2 else NG):
-                    if g == 0 and SPLIT0:
-                        nc.scalar.copy(out=wbc[:, g, 0, :], in_=raw[n][:, g, 0, :].bitcast(FP8))
-                        nc.vector.tensor_copy(out=wbc[:, g, 1, :], in_=raw[n][:, g, 1, :].bitcast(FP8))
-                        continue
-                    nc.scalar.copy(
-                        out=wbc[:, g, :, :].rearrange("p t k -> p (t k)"),
-                        in_=raw[n][:, g, :, :].rearrange("p t k -> p (t k)").bitcast(FP8),
-                    )
-                for t in tiles:
-                    words[(n, t)] = (wbc[:, :, t, :], "chunks")
-                return
-            wbs = {}
-            for t in tiles:
-                wbs[t] = work.tile([P, E], BF16, name="wb", tag="wb", bufs=6)
-            if n in Q_ON_VECTOR:
-                for t in tiles:
-                    nc.vector.tensor_scalar(
-                        out=wbs[t][:].rearrange("p (u w e) -> p w u e", u=2, e=2),
-                        in0=raw[(n, t)].bitcast(FP8).rearrange("p (w u e) -> p w u e", u=2, e=2),
-                        scalar1=ones[:, 0:1], scalar2=None, op0=MULT,
-                    )
-                    words[(n, t)] = (wbs[t][:].bitcast(F32), "ugp")
-                return
-            for t in tiles:
-                if (n, t) in V_WIDE:
-                    nc.vector.tensor_copy(out=wbs[t][:], in_=raw[(n, t)].bitcast(FP8))
-                else:
-                    nc.scalar.copy(out=wbs[t][:], in_=raw[(n, t)].bitcast(FP8))
-            for t in tiles:
-                if (n, t) in Q_ORDERED:
-                    words[(n, t)] = (put_in_order(wbs[t][:].bitcast(F32), "wpq"), True)
-                else:
-                    words[(n, t)] = (wbs[t][:].bitcast(F32), False)
-
-        def transpose_tile(w2, t, g, tp):
-            for u in range(2):
-                nc.tensor.transpose(tp[:, 256 * t + u:256 * t + 256:2], w2[t][0][:, 256 * g + u:256 * (g + 1):2], ident_f[:])
-
-        def transpose_bank(w2, g, bank):
-            tp = psum.tile([P, 512], F32, name=bank, tag=bank)
-            stepped = w2[0][1] is not True or w2[1][1] is not True
-            for t in range(2):
-                w, ordered = w2[t]
-                for u in range(2):
-                    if ordered == "ugp":
-                        src = w[:, 512 * u + 128 * g:512 * u + 128 * g + 128]
-                    elif ordered == "chunks":
-                        src = w[:, g, :].bitcast(F32)[:, u:256:2]
-                    elif ordered:
-                        src = w[:, 256 * g + 128 * u:256 * g + 128 * u + 128]
-                    else:
-                        src = w[:, 256 * g + u:256 * (g + 1):2]
-                    c0 = 256 * u + 128 * t
-                    dst = tp[:, 256 * t + u:256 * t + 256:2] if stepped else tp[:, c0:c0 + 128]
-                    nc.tensor.transpose(dst, src, ident_f[:])
-            return tp, stepped
-
-        def new_grp():
-            return work.tile([P, 4 * 1024], BF16, name="grp", tag="grp", bufs=4, align_bytes=64)
-
-        def by_row(bank):
-            tp, stepped = bank
-            return tp[:].rearrange("p (r u) -> p r u", u=2) if stepped else tp[:].rearrange("p (u r) -> p r u", u=2)
-
-        def copy_out_plain(bank, gt, c0, on_vector=False):
-            dst = gt[:, c0:c0 + 1024].bitcast(F32).rearrange("p (r u) -> p r u", u=2)
-            if on_vector:
-                nc.vector.tensor_copy(out=dst, in_=by_row(bank))
+            wide = work.tile([P, E], BF16, name="wide", tag="wide", bufs=6)
+            nc.scalar.copy(out=wide[:], in_=weights[(n, t)].bitcast(FP8))
+            if n >= FIRST_ORDERED and t == 0:
+                words[(n, t)] = (order_words(wide[:].bitcast(F32), "ordered_q", 2), True)
             else:
-                nc.scalar.copy(out=dst, in_=by_row(bank))
+                words[(n, t)] = (wide[:].bitcast(F32), False)
 
-        def copy_out_scaled(bank, gt, g):
-            tp, stepped = bank
-            dst = gt[:, 1024 * g:1024 * (g + 1)]
-            s4 = scl[:, 4 * g:4 * g + 4]
-            if stepped:
-                nc.vector.tensor_tensor(
-                    out=dst.rearrange("p (r t) -> p r t", t=4),
-                    in0=tp[:].bitcast(BF16).rearrange("p (r t) -> p r t", t=4),
-                    in1=s4.rearrange("p (o t) -> p o t", o=1).to_broadcast([P, 256, 4]),
-                    op=MULT,
-                )
+        def words_of_pass(w, ordered, g, u):
+            if ordered:
+                return w[:, 256 * g + 128 * u:256 * g + 128 * u + 128]
+            return w[:, 256 * g + u:256 * (g + 1):2]
+
+        def transpose_pass(dst, tiles):
+            by_row = not (tiles[0][2] and tiles[1][2])
+            for t in range(2):
+                for u in range(2):
+                    if by_row:
+                        out = dst[:, 256 * t + u:256 * t + 256:2]
+                    else:
+                        out = dst[:, 256 * u + 128 * t:256 * u + 128 * t + 128]
+                    nc.tensor.transpose(out, tiles[t][u], ident_f[:])
+            return by_row
+
+        def row_tile(n, t, g):
+            w, ordered = words[(n, t)]
+            return (words_of_pass(w, ordered, g, 0), words_of_pass(w, ordered, g, 1), ordered)
+
+        def new_group():
+            return work.tile([P, NG * UW * 4], BF16, name="group", tag="group", bufs=4, align_bytes=64)
+
+        def empty_bank(copy, src, by_row, group, c0):
+            order = "p (r u) -> p r u" if by_row else "p (u r) -> p r u"
+            copy(
+                out=group[:, c0:c0 + 1024].bitcast(F32).rearrange("p (r u) -> p r u", u=2),
+                in_=src[:].rearrange(order, u=2),
+            )
+
+        def turn(n, g):
+            dst = bank("tp%d" % g)
+            by_row = transpose_pass(dst, [row_tile(n, t, g) for t in range(2)])
+            turned[(n, g)] = dst
+            if UNITS[n][0] != "q":
+                if g == 0:
+                    groups[n] = new_group()
+                empty_bank(nc.scalar.copy, dst, by_row, groups[n], 1024 * g)
+
+        def turn_first_k():
+            for g in range(NG):
+                turned[(FIRST_K, g)] = bank("tp%d" % g)
+            for t in range(2):
+                w = weights[(FIRST_K, t)].bitcast(F32)
+                for g in range(NG):
+                    for u in range(2):
+                        nc.tensor.transpose(
+                            turned[(FIRST_K, g)][:, 256 * t + u:256 * t + 256:2], words_of_pass(w, False, g, u), ident_f[:]
+                        )
+
+        def fill(n, g):
+            if g == 0:
+                groups[n] = new_group()
+            if n == FIRST_K:
+                empty_bank(nc.vector.tensor_copy, turned[(n, g)], True, groups[n], 1024 * g)
                 return
             nc.vector.tensor_tensor(
-                out=dst.rearrange("p (r u e) -> p r u e", u=2, e=2),
-                in0=tp[:].bitcast(BF16).rearrange("p (u r e) -> p r u e", u=2, e=2),
-                in1=s4.rearrange("p (o u e) -> p o u e", o=1, u=2).to_broadcast([P, 256, 2, 2]),
+                out=groups[n][:, 1024 * g:1024 * (g + 1)].rearrange("p (r t) -> p r t", t=4),
+                in0=turned[(n, g)][:].bitcast(BF16).rearrange("p (r t) -> p r t", t=4),
+                in1=scales[:, 4 * g:4 * g + 4].rearrange("p (o t) -> p o t", o=1).to_broadcast([P, UW, 4]),
                 op=MULT,
             )
 
-        def tr(n, g):
-            if n in KSPLIT:
-                if g == NG - 1:
-                    for k in range(NG):
-                        tpt[(n, k)] = (psum.tile([P, 512], F32, name="tp%d" % k, tag="tp%d" % k), True)
-                    for t in range(2):
-                        for k in range(NG):
-                            transpose_tile((words[(n, 0)], words[(n, 1)]), t, k, tpt[(n, k)][0])
-                return
-            tpt[(n, g)] = transpose_bank((words[(n, 0)], words[(n, 1)]), g, "tp%d" % g)
-            if UNITS[n][0] != "q" and n not in VCOPY:
-                if g == 0:
-                    grp[n] = new_grp()
-                copy_out_plain(tpt[(n, g)], grp[n], 1024 * g, (n, g) in VTR)
-
-        def co(n, g):
-            if UNITS[n][0] == "q":
-                if g == 0:
-                    grp[n] = new_grp()
-                copy_out_scaled(tpt[(n, g)], grp[n], g)
-            elif n in VCOPY:
-                if g == 0:
-                    grp[n] = new_grp()
-                copy_out_plain(tpt[(n, g)], grp[n], 1024 * g, True)
-
-        def quantize(gt, c, s):
-            nc.vector.quantize_mx(out=c[:].bitcast(FP8X4), scales=s[:], in_=gt[:])
-
-        def qz(n):
-            c = work.tile([P, 1024], U32, name="wc", tag="wc", bufs=3, align_bytes=64)
-            s = work.tile([P, 1024], U8, name="ws", tag="ws", bufs=3, align_bytes=64)
-            quantize(grp[n], c, s)
+        def quantize(n):
+            c = work.tile([P, NG * UW], U32, name="codes", tag="codes", bufs=3, align_bytes=64)
+            s = work.tile([P, NG * UW], U8, name="planes", tag="planes", bufs=3, align_bytes=64)
+            nc.vector.quantize_mx(out=c[:].bitcast(FP8X4), scales=s[:], in_=groups[n][:])
             codes[n] = (c, s)
 
-        def head_of(n, hh):
-            kind, a = UNITS[n]
-            return 2 * a + hh + (0 if kind == "q" else 16)
+        sums = {}
+        products = {}
+        back = {}
 
-        def mm_ev(n, hh):
+        def x_operand(g, token0, tokens):
+            cols = slice(512 * (g % 2) + token0, 512 * (g % 2) + token0 + tokens)
+            return x_codes[g // 2][:, cols].bitcast(FP8X4), x_planes[g // 2][:, cols]
+
+        def w_operand(n, g, row0, rows):
             c, s = codes[n]
-            acc = psum.tile([P, 512], F32, name="ac%d" % hh, tag="ac%d" % hh)
+            cols = slice(UW * g + row0, UW * g + row0 + rows)
+            return c[:, cols].bitcast(FP8X4), s[:, cols]
+
+        def accumulate(out, stationary, moving):
             for g in range(NG):
-                wcol = slice(256 * g + 128 * hh, 256 * g + 128 * hh + 128)
-                xcol = slice(512 * (g % 2), 512 * (g % 2) + 512)
+                lhs, lhs_plane = stationary(g)
+                rhs, rhs_plane = moving(g)
                 nc.tensor.matmul_mx(
-                    out=acc[:],
-                    lhsT=c[:, wcol].bitcast(FP8X4),
-                    lhsT_scale=s[:, wcol],
-                    rhs=xc[g // 2][:, xcol].bitcast(FP8X4),
-                    rhs_scale=xs[g // 2][:, xcol],
-                    start=(g == 0),
-                    stop=(g == NG - 1),
-                )
-            accs[(n, hh)] = acc
-
-        def rope_v(n, hh):
-                acc = accs[(n, hh)]
-                h = head_of(n, hh)
-                t12 = work.tile([P, 1024], F32, name="t12", tag="t12", bufs=2 + 2 * LAG)
-                eps[(n, hh)] = t12
-                nc.vector.scalar_tensor_tensor(
-                    out=t12[:].rearrange("p (z c) -> p z c", z=2),
-                    in0=acc[:].rearrange("p (o c) -> p o c", o=1).to_broadcast([P, 2, 512]),
-                    scalar=bcol[:, h:h + 1],
-                    in1=tbT[:].rearrange("p (z c) -> p z c", z=2),
-                    op0=ADD, op1=MULT,
+                    out=out, lhsT=lhs, lhsT_scale=lhs_plane, rhs=rhs, rhs_scale=rhs_plane,
+                    start=(g == 0), stop=(g == NG - 1),
                 )
 
-        avs = {}
+        def multiply_head(n, h):
+            sums[(n, h)] = bank("ac%d" % h)
+            accumulate(
+                sums[(n, h)][:], lambda g: w_operand(n, g, P * h, P), lambda g: x_operand(g, 0, NT * P)
+            )
 
-        def rope_g(n, hh):
-            if n not in GPAIR:
-                rope_g1(n, hh)
-                return
-            if hh == 0:
-                avs[n] = work.tile([P, 1024], F32, name="av2", tag="av2", bufs=AV2)
-            h = head_of(n, hh)
-            nc.scalar.activation(out=avs[n][:, 512 * hh:512 * hh + 512], in_=accs[(n, hh)][:], func=IDENT, bias=bcol[:, h:h + 1], scale=1.0)
-            if hh == 1:
-                t2 = work.tile([P, 2048], F32, name="t22", tag="t22", bufs=T22)
-                nc.gpsimd.tensor_tensor(
-                    out=t2[:].rearrange("p (h z c) -> p h z c", h=2, z=2),
-                    in0=avs[n][:].rearrange("p (h o c) -> p h o c", h=2, o=1).to_broadcast([P, 2, 2, 512]),
-                    in1=tbT[:].rearrange("p (o z c) -> p o z c", o=1, z=2).to_broadcast([P, 2, 2, 512]),
-                    op=MULT,
+        def multiply_tokens(n, q, tags):
+            for j in range(2):
+                if j < len(tags):
+                    dst = bank(tags[j])
+                sums[(n, q, j)] = dst[:, UW * j:UW * j + UW]
+                accumulate(
+                    sums[(n, q, j)], lambda g: x_operand(g, P * (2 * q + j), P), lambda g: w_operand(n, g, 0, UW)
                 )
-                for k in range(2):
-                    eps[(n, k)] = t2[:, 1024 * k:1024 * k + 1024]
+            sums[(n, q)] = dst
 
-        def rope_g1(n, hh):
-            acc = accs[(n, hh)]
-            h = head_of(n, hh)
-            t12 = work.tile([P, 1024], F32, name="t12", tag="t12", bufs=2 + 2 * LAG)
-            av = work.tile([P, 512], F32, name="av", tag="av", bufs=2 + 2 * LAG)
-            nc.scalar.activation(out=av[:], in_=acc[:], func=IDENT, bias=bcol[:, h:h + 1], scale=1.0)
+        def new_products():
+            return work.tile([P, 1024], F32, name="products", tag="products", bufs=4)
+
+        def new_biased():
+            return work.tile([P, BANK], F32, name="biased", tag="biased", bufs=4)
+
+        def new_output():
+            return work.tile([P, BANK], F32, name="output", tag="output", bufs=6)
+
+        def head_bias(n, h):
+            kind, a = UNITS[n]
+            column = 2 * a + h + (0 if kind == "q" else 16)
+            return bias_cols[:, column:column + 1]
+
+        def rotate_head(n, h):
+            biased = new_biased()
+            products[(n, h)] = new_products()
+            nc.scalar.activation(out=biased[:], in_=sums[(n, h)][:], func=IDENT, bias=head_bias(n, h), scale=1.0)
             nc.gpsimd.tensor_tensor(
-                out=t12[:].rearrange("p (z c) -> p z c", z=2),
-                in0=av[:].rearrange("p (o c) -> p o c", o=1).to_broadcast([P, 2, 512]),
-                in1=tbT[:].rearrange("p (z c) -> p z c", z=2),
+                out=products[(n, h)][:].rearrange("p (z c) -> p z c", z=2),
+                in0=biased[:].rearrange("p (o c) -> p o c", o=1).to_broadcast([P, 2, BANK]),
+                in1=tables[:].rearrange("p (z c) -> p z c", z=2),
                 op=MULT,
             )
-            eps[(n, hh)] = t12
 
-        def mm_v(n, ip):
-            c, s = codes[n]
-            if not (TAILB and n == nu - 1):
-                acc = psum.tile([P, 512], F32, name="ac%d" % ip, tag="ac%d" % ip)
-            for il in range(2):
-                if TAILB and n == nu - 1:
-                    b1 = "tp%d" % (2 * ip + il)
-                    acc = psum.tile([P, 512], F32, name=b1, tag=b1)
-                    accs[(n, ip, il)] = acc
-                for g in range(NG):
-                    x0 = 512 * (g % 2) + 128 * (2 * ip + il)
-                    wcol = slice(256 * g, 256 * g + 256)
-                    nc.tensor.matmul_mx(
-                        out=acc[:, 256 * il:256 * il + 256],
-                        lhsT=xc[g // 2][:, x0:x0 + 128].bitcast(FP8X4),
-                        lhsT_scale=xs[g // 2][:, x0:x0 + 128],
-                        rhs=c[:, wcol].bitcast(FP8X4),
-                        rhs_scale=s[:, wcol],
-                        start=(g == 0),
-                        stop=(g == NG - 1),
-                    )
-            accs[(n, ip)] = acc
-
-        def rope_x(n, ip):
-            a = UNITS[n][1]
-            av = work.tile([P, 512], F32, name="av", tag="av", bufs=2 + 2 * LAG)
-            nc.vector.tensor_tensor(
-                out=av[:].rearrange("p (i f) -> p i f", i=2),
-                in0=accs[(n, ip)][:].rearrange("p (i f) -> p i f", i=2),
-                in1=bbx[n][:].rearrange("p (o f) -> p o f", o=1).to_broadcast([P, 2, UW]),
-                op=ADD,
+        def rotate_head_on_vector(n, h):
+            products[(n, h)] = new_products()
+            nc.vector.scalar_tensor_tensor(
+                out=products[(n, h)][:].rearrange("p (z c) -> p z c", z=2),
+                in0=sums[(n, h)][:].rearrange("p (o c) -> p o c", o=1).to_broadcast([P, 2, BANK]),
+                scalar=head_bias(n, h),
+                in1=tables[:].rearrange("p (z c) -> p z c", z=2),
+                op0=ADD, op1=MULT,
             )
-            avx[(n, ip)] = av
-            if not TBL:
-                prod_x(n, ip)
 
-        avx = {}
-
-        def prod_x(n, ip):
-            av = avx[(n, ip)]
-            t12 = work.tile([P, 1024], F32, name="t12", tag="t12", bufs=2 + 2 * LAG)
-            for il in range(2):
-                (nc.vector if (n, ip) in XV else nc.gpsimd).tensor_tensor(
-                    out=t12[:, 512 * il:512 * il + 512].rearrange("p (z h f) -> p z h f", z=2, h=2),
-                    in0=av[:, 256 * il:256 * il + 256].rearrange("p (o h f) -> p o h f", o=1, h=2).to_broadcast([P, 2, 2, P]),
-                    in1=cs_sb[:, 2 * ip + il, :, :].rearrange("p z (o f) -> p z o f", o=1).to_broadcast([P, 2, 2, P]),
-                    op=MULT,
-                )
-            eps[(n, ip)] = t12
-
-        def fin_x(n, ip):
-            a = UNITS[n][1]
-            t = eps[(n, ip)][:].rearrange("p (i z h w f) -> p i z h w f", i=2, z=2, h=2, w=2)
-            o = work.tile([P, 512], F32, name="o", tag="o", bufs=OB)
-            for il in range(2):
-                nc.vector.tensor_tensor(
-                    out=o[:].rearrange("p (h i w f) -> p i h w f", h=2, i=2, w=2)[:, il, :, :, :],
-                    in0=t[:, il, 0, :, :, :],
-                    in1=t[:, il, 1, :, ::-1, :],
-                    op=ADD,
-                )
-            store_rows(UNITS[n][0], a, ip, o)
-
-        def store_rows(kind, a, ip, o, ils=(0, 1)):
-            dst = outs[kind][2 * a:2 * a + 2, :, :]
-            if len(ils) == 2:
-                nc.sync.dma_start(
-                    out=dst.rearrange("h (p q i) f -> q p h (i f)", q=2, i=2)[ip],
-                    in_=o[:].rearrange("p (h c) -> p h c", h=2),
-                )
-                return
-            for il in ils:
-                nc.sync.dma_start(
-                    out=dst.rearrange("h (p q i) f -> q i p h f", q=2, i=2)[ip, il],
-                    in_=o[:].rearrange("p (h i f) -> p h i f", h=2, i=2)[:, :, il, :],
-                )
-
-        def fin_v(n, ip):
-            a = UNITS[n][1]
-            o = work.tile([P, 512], F32, name="o", tag="o", bufs=OB)
-            if TAILB and n == nu - 1:
-                for il in range(2):
-                    col = slice(UW * il, UW * il + UW)
-                    nc.vector.tensor_tensor(
-                        out=o[:].rearrange("p (h i f) -> p h i f", h=2, i=2)[:, :, il, :],
-                        in0=accs[(n, ip, il)][:, col].rearrange("p (h f) -> p h f", h=2),
-                        in1=bbv[:, UW * a:UW * a + UW].rearrange("p (h f) -> p h f", h=2),
-                        op=ADD,
-                    )
-                    store_rows("v", a, ip, o, (il,))
-                return
-            nc.vector.tensor_tensor(
-                out=o[:].rearrange("p (h i f) -> p i h f", h=2, i=2),
-                in0=accs[(n, ip)][:].rearrange("p (i h f) -> p i h f", i=2, h=2),
-                in1=bbv[:, UW * a:UW * a + UW].rearrange("p (o h f) -> p o h f", o=1, h=2).to_broadcast([P, 2, 2, P]),
-                op=ADD,
-            )
-            store_rows("v", a, ip, o)
-
-        def bt(n, hh):
-            t = eps[(n, hh)] if n in GPAIR else eps[(n, hh)][:]
-            ob = psum.tile([P, 512], F32, name="ob%d" % hh, tag="ob%d" % hh)
-            for i in range(4):
-                col = slice(128 * i, 128 * i + 128)
-                nc.tensor.matmul(out=ob[:, col], lhsT=t[:, col], rhs=ident_f[:], is_transpose=True, start=True, stop=False)
+        def turn_back(n, h):
+            src = products[(n, h)]
+            dst = bank("ob%d" % h)
+            for i in range(NT):
+                col = slice(P * i, P * i + P)
+                nc.tensor.matmul(out=dst[:, col], lhsT=src[:, col], rhs=ident_f[:], is_transpose=True, start=True, stop=False)
                 nc.tensor.matmul(
-                    out=ob[:, col], lhsT=t[:, 512 + 128 * i:640 + 128 * i], rhs=swap_f[:],
+                    out=dst[:, col], lhsT=src[:, BANK + P * i:BANK + P * i + P], rhs=swap_f[:],
                     is_transpose=True, start=False, stop=True,
                 )
-            obs[(n, hh)] = ob
+            back[(n, h)] = dst
 
-        def fin(n, hh):
+        def store_head(n, h, copy):
             kind, a = UNITS[n]
-            o = work.tile([P, 512], F32, name="o", tag="o", bufs=OB)
-            if (n, hh) in FINV:
-                nc.vector.tensor_copy(out=o[:], in_=obs[(n, hh)][:])
-            else:
-                nc.scalar.copy(out=o[:], in_=obs[(n, hh)][:])
+            o = new_output()
+            copy(out=o[:], in_=back[(n, h)][:])
             nc.sync.dma_start(
-                out=outs[kind][2 * a + hh, :, :].rearrange("(p i) f -> p (i f)", i=4),
-                in_=o[:],
+                out=outs[kind][2 * a + h, :, :].rearrange("(i p) f -> p i f", p=P),
+                in_=o[:].rearrange("p (i f) -> p i f", i=NT),
             )
 
-        def tables():
-            zt_ps = psum.tile([P, P], BF16, name="ob0", tag="ob0")
-            nc.tensor.transpose(zt_ps[:], zb[:], ident_b[:])
-            nc.scalar.copy(out=bcol[:], in_=zt_ps[:, 0:24])
-            tb_ps = psum.tile([P, 1024], BF16, name="ob1", tag="ob1")
-            for z in range(2):
-                for i in range(4):
-                    nc.tensor.transpose(tb_ps[:, 512 * z + 128 * i:512 * z + 128 * i + 128], cs_sb[:, i, z, :], ident_b[:])
-            nc.scalar.copy(out=tbT[:], in_=tb_ps[:])
+        def rotate_tokens(n, q):
+            biased = new_biased()
+            nc.vector.tensor_tensor(
+                out=biased[:].rearrange("p (j f) -> p j f", j=2),
+                in0=sums[(n, q)][:].rearrange("p (j f) -> p j f", j=2),
+                in1=bias_q[:].rearrange("p (o f) -> p o f", o=1).to_broadcast([P, 2, UW]),
+                op=ADD,
+            )
+            products[(n, q)] = new_products()
+            for j in range(2):
+                nc.vector.tensor_tensor(
+                    out=products[(n, q)][:, BANK * j:BANK * j + BANK].rearrange("p (z h f) -> p z h f", z=2, h=2),
+                    in0=biased[:, UW * j:UW * j + UW].rearrange("p (o h f) -> p o h f", o=1, h=2).to_broadcast([P, 2, 2, P]),
+                    in1=cs[:, 2 * q + j, :, :].rearrange("p z (o f) -> p z o f", o=1).to_broadcast([P, 2, 2, P]),
+                    op=MULT,
+                )
 
-        cast(0)
+        def store_tile(n, i, src):
+            kind, a = UNITS[n]
+            nc.sync.dma_start(
+                out=outs[kind][2 * a:2 * a + 2, P * i:P * i + P, :].rearrange("h p f -> p h f"),
+                in_=src.rearrange("p (h f) -> p h f", h=2),
+            )
+
+        def add_and_store_tokens(n, q):
+            src = products[(n, q)][:].rearrange("p (j z h w f) -> p j z h w f", j=2, z=2, h=2, w=2)
+            o = new_output()
+            for j in range(2):
+                nc.vector.tensor_tensor(
+                    out=o[:, UW * j:UW * j + UW].rearrange("p (h w f) -> p h w f", h=2, w=2),
+                    in0=src[:, j, 0, :, :, :],
+                    in1=src[:, j, 1, :, ::-1, :],
+                    op=ADD,
+                )
+            for j in range(2):
+                store_tile(n, 2 * q + j, o[:, UW * j:UW * j + UW])
+
+        def finish_v(n, q):
+            a = UNITS[n][1]
+            o = new_output()
+            nc.vector.tensor_tensor(
+                out=o[:].rearrange("p (j f) -> p j f", j=2),
+                in0=sums[(n, q)][:].rearrange("p (j f) -> p j f", j=2),
+                in1=bias_v[:, UW * a:UW * a + UW].rearrange("p (o f) -> p o f", o=1).to_broadcast([P, 2, UW]),
+                op=ADD,
+            )
+            for j in range(2):
+                store_tile(n, 2 * q + j, o[:, UW * j:UW * j + UW])
+
+        def finish_last_v(q):
+            a = UNITS[LAST_V][1]
+            o = new_output()
+            for j in range(2):
+                part = o[:, UW * j:UW * j + UW]
+                nc.vector.tensor_tensor(out=part, in0=sums[(LAST_V, q, j)], in1=bias_v[:, UW * a:UW * a + UW], op=ADD)
+                store_tile(LAST_V, 2 * q + j, part)
+
+        wide_first = work.tile([P, NG, 2, 512], BF16, name="wide_first", tag="wide_first", bufs=1)
         for g in range(NG):
-            tr(0, g)
-        if HEADK:
-            cast(1)
-            for g in range(NG):
-                co(0, g)
-                tr(1, g)
-            qz(0)
-        xc = []
-        xs = []
-        xg = [new_grp(), new_grp()]
-        xbanks = ("ac0", "ac1", "ob0", "ob1")
-        if X_SINGLE:
-            for i in range(4):
-                xw = x_sb[i][:].bitcast(F32)
-                for j in range(2):
-                    b1 = xbanks[(2 * i + j) % 4]
-                    tp = psum.tile([P, 512], F32, name=b1, tag=b1)
-                    for pp in range(2):
-                        for u in range(2):
-                            c0 = 256 * (2 * j + pp)
-                            nc.tensor.transpose(tp[:, 256 * pp + u:256 * pp + 256:2], xw[:, c0 + u:c0 + 256:2], ident_f[:])
-                    nc.scalar.copy(
-                        out=xg[j][:].bitcast(F32).rearrange("p (q c) -> p q c", q=2)[:, :, 256 * i:256 * i + 256],
-                        in_=tp[:].rearrange("p (q c) -> p q c", q=2),
-                    )
-        for ip in range(0 if X_SINGLE else 2):
-            for g in range(NG):
-                tp = transpose_bank(((x_sb[2 * ip][:].bitcast(F32), False), (x_sb[2 * ip + 1][:].bitcast(F32), False)), g, xbanks[g])
-                copy_out_plain(tp, xg[g // 2], 2048 * (g % 2) + 1024 * ip)
-        if not HEADK:
-            cast(1)
-        bcol = const.tile([P, 24], F32, name="bcol")
-        tbT = const.tile([P, 1024], BF16, name="tbT")
+            for t in range(2):
+                widen = nc.vector.tensor_copy if (g, t) == (0, 1) else nc.scalar.copy
+                widen(out=wide_first[:, g, t, :], in_=wq_first[g][:, t, :].bitcast(FP8))
+        for g in range(NG):
+            turned[(FIRST_Q, g)] = bank("tp%d" % g)
+            tiles = []
+            for t in range(2):
+                w = wide_first[:, g, t, :].bitcast(F32)
+                tiles.append((w[:, 0:256:2], w[:, 1:256:2], False))
+            transpose_pass(turned[(FIRST_Q, g)], tiles)
 
-        def mm_half(s, half):
-            if UNITS[s][0] == "v" or s in XK:
-                mm_v(s, half)
-            else:
-                mm_ev(s, half)
-                if s == 0 and half == 0:
-                    tables()
-                if (s, half) not in V_HEADS:
-                    rope_g(s, half)
+        x_groups = [new_group(), new_group()]
+        for q in range(2):
+            for g in range(NG):
+                dst = bank(("ac0", "ac1", "ob0", "ob1")[g])
+                tiles = []
+                for t in range(2):
+                    w = x_sb[2 * q + t][:].bitcast(F32)
+                    tiles.append((words_of_pass(w, False, g, 0), words_of_pass(w, False, g, 1), False))
+                transpose_pass(dst, tiles)
+                empty_bank(nc.scalar.copy, dst, True, x_groups[g // 2], 2048 * (g % 2) + 1024 * q)
+        bias_cols = const.tile([P, 24], F32, name="bias_cols")
+        tables = const.tile([P, 2 * BANK], BF16, name="tables")
 
-        pre = [(n, t) for n in range(nu) if UNITS[n][0] != "q" and n not in KV_AS_LOADED for t in range(2)]
-        back = {}
-        for n in range(nu):
-            if UNITS[n][0] != "v" and n not in XK:
-                back.setdefault(n + (2 if n in LAG2 else 1), []).append(n)
-        for s in range(-1, 8 if TBL else nu + 2):
-            late = s in Q_LATE
-            if s in Q_EARLY and (s not in XK or not QX):
-                qz(s + 1)
-            for half in range(2):
-                if 0 <= s < nu and not late and s not in MERGE:
-                    mm_half(s, half)
-                if s in MERGE and half == 0:
-                    mm_half(s, 0)
-                    mm_half(s, 1)
-                if s in XK:
-                    rope_x(s, half)
-                    if half == 0 and QX:
-                        qz(s + 1)
-                if s + 3 < nu and (UNITS[s + 3][0] == "q" or s + 3 in KV_AS_LOADED or not PRE):
-                    cast(s + 3, (half,))
-                if half == PRE_HALF and PRE and 0 <= s - PRE_AT < len(pre):
-                    cast(pre[s - PRE_AT][0], (pre[s - PRE_AT][1],))
-                for g in (2 * half, 2 * half + 1):
-                    if s + 1 < nu and not (HEADK and s == -1) and not (HEADK == 3 and s == 0):
-                        co(s + 1, g)
-                    if late and g == 0:
-                        qz(s)
-                    if s + 2 < nu and not (HEADK and s == -1):
-                        tr(s + 2, g)
-                if late:
-                    mm_half(s, half)
-                if half == 0 and (s, 0) in V_HEADS:
-                    rope_v(s, 0)
-                for b in back.get(s, ()):
-                    bt(b, half)
-                    if half == 0:
-                        fin(b, 0)
-            if s + 1 < nu and s not in Q_EARLY and s + 1 not in Q_LATE and not (HEADK and s == -1) and not (HEADK == 3 and s == 0):
-                qz(s + 1)
-            if (s, 1) in V_HEADS:
-                rope_v(s, 1)
-            if s == -1 and HEADK == 3:
+        x_codes = []
+        x_planes = []
+
+        def quantize_x():
+            for j in range(2):
+                x_codes.append(const.tile([P, 1024], U32, name="x_codes%d" % j, align_bytes=64))
+                x_planes.append(const.tile([P, 1024], U8, name="x_planes%d" % j, align_bytes=64))
+            for q in range(2):
                 for g in range(NG):
-                    co(1, g)
-                if not Q1_LAST:
-                    qz(1)
-            if s == -1:
-                for gp in range(2):
-                    c = const.tile([P, 1024], U32, name="xc%d" % gp, align_bytes=64)
-                    sc = const.tile([P, 1024], U8, name="xs%d" % gp, align_bytes=64)
-                    if not XQ_SPLIT:
-                        quantize(xg[gp], c, sc)
-                    xc.append(c)
-                    xs.append(sc)
-                for ip in range(2 if XQ_SPLIT else 0):
-                    for g in range(NG):
-                        c0 = 512 * (g % 2) + 256 * ip
-                        nc.vector.quantize_mx(
-                            out=xc[g // 2][:, c0:c0 + 256].bitcast(FP8X4),
-                            scales=xs[g // 2][:, c0:c0 + 256],
-                            in_=xg[g // 2][:, 4 * c0:4 * c0 + 1024],
-                        )
-                if HEADK == 3 and Q1_LAST:
-                    qz(1)
-            for ip in range(2):
-                if s - XLAG[ip] in XK and XPRE[ip]:
-                    fin_x(s - XLAG[ip], ip)
-            if 0 <= s < nu and UNITS[s][0] == "v":
-                fin_v(s, 0)
-                fin_v(s, 1)
-            for ip in range(2):
-                if s - XLAG[ip] in XK and not XPRE[ip]:
-                    fin_x(s - XLAG[ip], ip)
-            for b in back.get(s, ()):
-                fin(b, 1)
-        def act(item):
-            k = item[0]
-            if k == "q":
-                qz(item[1])
-            elif k == "bias":
-                rope_x(item[1], item[2])
-            elif k == "prod":
-                prod_x(item[1], item[2])
-            elif k == "add":
-                fin_x(item[1], item[2])
-            elif k == "finv":
-                fin_v(item[1], item[2])
-            elif k == "stt":
-                rope_v(item[1], item[2])
-            elif k == "fin":
-                fin(item[1], item[2])
+                    col = 512 * (g % 2) + 256 * q
+                    nc.vector.quantize_mx(
+                        out=x_codes[g // 2][:, col:col + 256].bitcast(FP8X4),
+                        scales=x_planes[g // 2][:, col:col + 256],
+                        in_=x_groups[g // 2][:, 4 * col:4 * col + 1024],
+                    )
 
-        for s in range(8, nu + 1) if TBL else ():
-            def slot(j):
-                for it in TBL.get((s, j), ()):
-                    act(it)
-            slot(0)
+        def make_tables():
+            dst = psum.tile([P, P], BF16, name="ob0", tag="ob0")
+            nc.tensor.transpose(dst[:], bias_rows[:], ident_b[:])
+            nc.scalar.copy(out=bias_cols[:], in_=dst[:, 0:24])
+            dst = psum.tile([P, 2 * BANK], BF16, name="ob1", tag="ob1")
+            for z in range(2):
+                for i in range(NT):
+                    col = BANK * z + P * i
+                    nc.tensor.transpose(dst[:, col:col + P], cs[:, i, z, :], ident_b[:])
+            nc.scalar.copy(out=tables[:], in_=dst[:])
+
+        for s in range(-1, LAST_Q):
             for half in range(2):
-                if s < nu:
-                    mm_half(s, half)
-                slot(4 * half + 1)
-                if s + 3 < nu:
-                    cast(s + 3, (half,))
+                if s >= 0:
+                    multiply_head(s, half)
+                    if s == 0 and half == 0:
+                        make_tables()
+                    if (s, half) != (LAST_Q - 1, 1):
+                        rotate_head(s, half)
+                prepare(s + 3, half)
                 for g in (2 * half, 2 * half + 1):
-                    if s + 2 < nu:
-                        tr(s + 2, g)
-                slot(4 * half + 2)
-                for b in back.get(s, ()):
-                    bt(b, half)
-                slot(4 * half + 3)
-            slot(8)
+                    if UNITS[s + 1][0] == "q" or s + 1 == FIRST_K:
+                        fill(s + 1, g)
+                    if s + 2 == FIRST_K:
+                        if g == NG - 1:
+                            turn_first_k()
+                    else:
+                        turn(s + 2, g)
+                if s >= 1:
+                    turn_back(s - 1, half)
+                    if half == 0:
+                        store_head(s - 1, 0, nc.scalar.copy)
+            quantize(s + 1)
+            if s == -1:
+                quantize_x()
+            if s == LAST_Q - 1:
+                rotate_head_on_vector(s, 1)
+            if s >= 1:
+                store_head(s - 1, 1, nc.scalar.copy)
+
+        for half in range(2):
+            multiply_tokens(LAST_Q, half, ("ac%d" % half,))
+            rotate_tokens(LAST_Q, half)
+            if half == 0:
+                quantize(LAST_K)
+            prepare(LAST_V, half)
+            for g in (2 * half, 2 * half + 1):
+                turn(FIRST_V, g)
+            turn_back(LAST_Q - 1, half)
+            if half == 0:
+                store_head(LAST_Q - 1, 0, nc.vector.tensor_copy)
+        store_head(LAST_Q - 1, 1, nc.scalar.copy)
+
+        quantize(FIRST_V)
+        for half in range(2):
+            multiply_head(LAST_K, half)
+            for g in (2 * half, 2 * half + 1):
+                turn(LAST_V, g)
+            rotate_head_on_vector(LAST_K, half)
+        for q in range(2):
+            add_and_store_tokens(LAST_Q, q)
+
+        for half in range(2):
+            multiply_tokens(FIRST_V, half, ("ac%d" % half,))
+            turn_back(LAST_K, half)
+            if half == 0:
+                store_head(LAST_K, 0, nc.scalar.copy)
+        quantize(LAST_V)
+        for q in range(2):
+            finish_v(FIRST_V, q)
+        store_head(LAST_K, 1, nc.scalar.copy)
+
+        for q in range(2):
+            multiply_tokens(LAST_V, q, ("tp%d" % (2 * q), "tp%d" % (2 * q + 1)))
+        for q in range(2):
+            finish_last_v(q)

from contextlib import ExitStack

import concourse.mybir as mybir
from concourse.masks import make_identity

FLOPS = 2 * 512 * 2048 * 3072

F32 = mybir.dt.float32
BF16 = mybir.dt.bfloat16
U32 = mybir.dt.uint32
U8 = mybir.dt.uint8
FP8 = mybir.dt.float8_e4m3fn
FP8X4 = mybir.dt.float8_e4m3fn_x4
MULT = mybir.AluOpType.mult
ADD = mybir.AluOpType.add
IDENT = mybir.ActivationFunctionType.Identity

P = 128
HALF = P // 2
E = 2048
NG = 4
UW = 256
NT = 4
BANK = 512

UNITS = (
    ("q", 0), ("k", 0), ("q", 1), ("q", 2), ("q", 3), ("q", 4),
    ("q", 5), ("q", 6), ("q", 7), ("k", 1), ("v", 0), ("v", 1),
)
NU = len(UNITS)
FIRST_Q, FIRST_K, LAST_Q, LAST_K, FIRST_V, LAST_V = 0, 1, 8, 9, 10, 11
FIRST_ORDERED = 4


def tile_qwen2attention_pa_kernel(
    tc, x, Wq_bytes, Wq_scale, bq, Wkv, bkv, cos, sin, out_0, out_1, out_2
):
    nc = tc.nc
    outs = {
        "q": out_0.rearrange("b h s f -> (b h) s f"),
        "k": out_1.rearrange("b h s f -> (b h) s f"),
        "v": out_2.rearrange("b h s f -> (b h) s f"),
    }

    with ExitStack() as ctx:
        const = ctx.enter_context(tc.tile_pool(name="const", bufs=1))
        loaded = ctx.enter_context(tc.tile_pool(name="loaded", bufs=1))
        work = ctx.enter_context(tc.tile_pool(name="work", bufs=2))
        psum = ctx.enter_context(tc.psum_pool(name="psum", bufs=1))
        ctx.enter_context(tc.manual_schedule())

        def bank(tag):
            return psum.tile([P, BANK], F32, name=tag, tag=tag)

        ident_f = const.tile([P, P], F32, name="ident_f")
        make_identity(nc, ident_f[:])
        ident_b = const.tile([P, P], BF16, name="ident_b")
        make_identity(nc, ident_b[:])
        swap_f = const.tile([P, P], F32, name="swap_f")
        nc.gpsimd.tensor_copy(out=swap_f[:, 0:HALF], in_=ident_f[:, HALF:P])
        nc.gpsimd.tensor_copy(out=swap_f[:, HALF:P], in_=ident_f[:, 0:HALF])

        warm = const.tile([P, 2], F32, name="warm")
        nc.vector.memset(warm[:, 0:1], 0.0)
        nc.scalar.copy(out=warm[:, 1:2], in_=warm[:, 0:1])
        bias_rows = const.tile([P, P], BF16, name="bias_rows")
        nc.vector.memset(bias_rows[:], 0.0)

        wq_first = {}
        weights = {}
        x_sb = []
        scales = const.tile([P, NG * 4], F32, name="scales")
        cs = const.tile([P, NT, 2, P], BF16, name="cs")

        def rows_of(n):
            kind, a = UNITS[n]
            if kind == "q":
                src = Wq_bytes[UW * a:UW * a + UW, :]
            else:
                row = UW * a + (512 if kind == "v" else 0)
                src = Wkv[row:row + UW, :]
            return src.rearrange("(t p) k -> p t k", p=P)

        def load_unit(n):
            tile = loaded.tile([P, 2, E], U8 if UNITS[n][0] == "q" else BF16, name="weights%d" % n)
            if n == FIRST_K:
                for t in range(2):
                    nc.sync.dma_start(out=tile[:, t, :], in_=rows_of(n)[:, t, :])
            else:
                nc.sync.dma_start(out=tile[:], in_=rows_of(n))
            for t in range(2):
                weights[(n, t)] = tile[:, t, :]

        for part, (k0, k1) in enumerate(((0, 512), (512, E))):
            tile = loaded.tile([P, 2, k1 - k0], U8, name="weights0_%d" % part)
            nc.sync.dma_start(out=tile[:], in_=rows_of(FIRST_Q)[:, :, k0:k1])
            for g in range(k0 // 512, k1 // 512):
                wq_first[g] = tile[:, :, 512 * g - k0:512 * g - k0 + 512]
        nc.sync.dma_start(
            out=scales[:].rearrange("p (g t) -> p g t", t=4),
            in_=Wq_scale.rearrange("o (g p t) -> p (o g) t", p=P, t=4),
        )
        x_rows = x.rearrange("b s k -> (b s) k")
        for i in range(NT):
            tile = loaded.tile([P, E], BF16, name="x%d" % i)
            nc.sync.dma_start(out=tile[:], in_=x_rows[P * i:P * i + P, :])
            x_sb.append(tile)
        load_unit(1)
        load_unit(2)
        nc.sync.dma_start(out=cs[:, :, 0, 0:HALF], in_=cos.rearrange("(i p) j -> p i j", p=P))
        nc.sync.dma_start(out=cs[:, :, 1, 0:HALF], in_=sin.rearrange("(i p) j -> p i j", p=P))
        nc.sync.dma_start(out=bias_rows[0:16, :], in_=bq.rearrange("(h f) -> h f", f=P))
        nc.sync.dma_start(out=bias_rows[16:24, :], in_=bkv.rearrange("(h f) -> h f", f=P))
        for n in range(3, NU):
            load_unit(n)
        bias_q = const.tile([P, UW], BF16, name="bias_q")
        a = UNITS[LAST_Q][1]
        nc.sync.dma_start(out=bias_q[:], in_=bq[UW * a:UW * a + UW].partition_broadcast(P))
        bias_v = const.tile([P, 2 * UW], BF16, name="bias_v")
        nc.sync.dma_start(out=bias_v[:], in_=bkv[512:1024].partition_broadcast(P))
        for z, sign in ((0, 1.0), (1, -1.0)):
            nc.gpsimd.tensor_scalar(
                out=cs[:, :, z, HALF:P], in0=cs[:, :, z, 0:HALF], scalar1=sign, scalar2=0.0, op0=MULT, op1=ADD
            )

        words = {}
        turned = {}
        groups = {}
        codes = {}

        def order_words(src, tag, bufs):
            dst = work.tile([P, E // 2], F32, name=tag, tag=tag, bufs=bufs)
            nc.scalar.copy(
                out=dst[:].rearrange("p (g u w) -> p g u w", g=NG, u=2),
                in_=src.rearrange("p (g w u) -> p g u w", g=NG, u=2),
            )
            return dst[:]

        def prepare(n, t):
            if UNITS[n][0] != "q":
                words[(n, t)] = (order_words(weights[(n, t)].bitcast(F32), "ordered_kv", 4), True)
                return
            wide = work.tile([P, E], BF16, name="wide", tag="wide", bufs=6)
            nc.scalar.copy(out=wide[:], in_=weights[(n, t)].bitcast(FP8))
            if n >= FIRST_ORDERED and t == 0:
                words[(n, t)] = (order_words(wide[:].bitcast(F32), "ordered_q", 2), True)
            else:
                words[(n, t)] = (wide[:].bitcast(F32), False)

        def words_of_pass(w, ordered, g, u):
            if ordered:
                return w[:, 256 * g + 128 * u:256 * g + 128 * u + 128]
            return w[:, 256 * g + u:256 * (g + 1):2]

        def transpose_pass(dst, tiles):
            by_row = not (tiles[0][2] and tiles[1][2])
            for t in range(2):
                for u in range(2):
                    if by_row:
                        out = dst[:, 256 * t + u:256 * t + 256:2]
                    else:
                        out = dst[:, 256 * u + 128 * t:256 * u + 128 * t + 128]
                    nc.tensor.transpose(out, tiles[t][u], ident_f[:])
            return by_row

        def row_tile(n, t, g):
            w, ordered = words[(n, t)]
            return (words_of_pass(w, ordered, g, 0), words_of_pass(w, ordered, g, 1), ordered)

        def new_group():
            return work.tile([P, NG * UW * 4], BF16, name="group", tag="group", bufs=4, align_bytes=64)

        def empty_bank(copy, src, by_row, group, c0):
            order = "p (r u) -> p r u" if by_row else "p (u r) -> p r u"
            copy(
                out=group[:, c0:c0 + 1024].bitcast(F32).rearrange("p (r u) -> p r u", u=2),
                in_=src[:].rearrange(order, u=2),
            )

        def turn(n, g):
            dst = bank("tp%d" % g)
            by_row = transpose_pass(dst, [row_tile(n, t, g) for t in range(2)])
            turned[(n, g)] = dst
            if UNITS[n][0] != "q":
                if g == 0:
                    groups[n] = new_group()
                empty_bank(nc.scalar.copy, dst, by_row, groups[n], 1024 * g)

        def turn_first_k():
            for g in range(NG):
                turned[(FIRST_K, g)] = bank("tp%d" % g)
            for t in range(2):
                w = weights[(FIRST_K, t)].bitcast(F32)
                for g in range(NG):
                    for u in range(2):
                        nc.tensor.transpose(
                            turned[(FIRST_K, g)][:, 256 * t + u:256 * t + 256:2], words_of_pass(w, False, g, u), ident_f[:]
                        )

        def fill(n, g):
            if g == 0:
                groups[n] = new_group()
            if n == FIRST_K:
                empty_bank(nc.vector.tensor_copy, turned[(n, g)], True, groups[n], 1024 * g)
                return
            nc.vector.tensor_tensor(
                out=groups[n][:, 1024 * g:1024 * (g + 1)].rearrange("p (r t) -> p r t", t=4),
                in0=turned[(n, g)][:].bitcast(BF16).rearrange("p (r t) -> p r t", t=4),
                in1=scales[:, 4 * g:4 * g + 4].rearrange("p (o t) -> p o t", o=1).to_broadcast([P, UW, 4]),
                op=MULT,
            )

        def quantize(n):
            c = work.tile([P, NG * UW], U32, name="codes", tag="codes", bufs=3, align_bytes=64)
            s = work.tile([P, NG * UW], U8, name="planes", tag="planes", bufs=3, align_bytes=64)
            nc.vector.quantize_mx(out=c[:].bitcast(FP8X4), scales=s[:], in_=groups[n][:])
            codes[n] = (c, s)

        sums = {}
        products = {}
        back = {}

        def x_operand(g, token0, tokens):
            cols = slice(512 * (g % 2) + token0, 512 * (g % 2) + token0 + tokens)
            return x_codes[g // 2][:, cols].bitcast(FP8X4), x_planes[g // 2][:, cols]

        def w_operand(n, g, row0, rows):
            c, s = codes[n]
            cols = slice(UW * g + row0, UW * g + row0 + rows)
            return c[:, cols].bitcast(FP8X4), s[:, cols]

        def accumulate(out, stationary, moving):
            for g in range(NG):
                lhs, lhs_plane = stationary(g)
                rhs, rhs_plane = moving(g)
                nc.tensor.matmul_mx(
                    out=out, lhsT=lhs, lhsT_scale=lhs_plane, rhs=rhs, rhs_scale=rhs_plane,
                    start=(g == 0), stop=(g == NG - 1),
                )

        def multiply_head(n, h):
            sums[(n, h)] = bank("ac%d" % h)
            accumulate(
                sums[(n, h)][:], lambda g: w_operand(n, g, P * h, P), lambda g: x_operand(g, 0, NT * P)
            )

        def multiply_tokens(n, q, tags):
            for j in range(2):
                if j < len(tags):
                    dst = bank(tags[j])
                sums[(n, q, j)] = dst[:, UW * j:UW * j + UW]
                accumulate(
                    sums[(n, q, j)], lambda g: x_operand(g, P * (2 * q + j), P), lambda g: w_operand(n, g, 0, UW)
                )
            sums[(n, q)] = dst

        def new_products():
            return work.tile([P, 1024], F32, name="products", tag="products", bufs=4)

        def new_biased():
            return work.tile([P, BANK], F32, name="biased", tag="biased", bufs=4)

        def new_output():
            return work.tile([P, BANK], F32, name="output", tag="output", bufs=6)

        def head_bias(n, h):
            kind, a = UNITS[n]
            column = 2 * a + h + (0 if kind == "q" else 16)
            return bias_cols[:, column:column + 1]

        def rotate_head(n, h):
            biased = new_biased()
            products[(n, h)] = new_products()
            nc.scalar.activation(out=biased[:], in_=sums[(n, h)][:], func=IDENT, bias=head_bias(n, h), scale=1.0)
            nc.gpsimd.tensor_tensor(
                out=products[(n, h)][:].rearrange("p (z c) -> p z c", z=2),
                in0=biased[:].rearrange("p (o c) -> p o c", o=1).to_broadcast([P, 2, BANK]),
                in1=tables[:].rearrange("p (z c) -> p z c", z=2),
                op=MULT,
            )

        def rotate_head_on_vector(n, h):
            products[(n, h)] = new_products()
            nc.vector.scalar_tensor_tensor(
                out=products[(n, h)][:].rearrange("p (z c) -> p z c", z=2),
                in0=sums[(n, h)][:].rearrange("p (o c) -> p o c", o=1).to_broadcast([P, 2, BANK]),
                scalar=head_bias(n, h),
                in1=tables[:].rearrange("p (z c) -> p z c", z=2),
                op0=ADD, op1=MULT,
            )

        def turn_back(n, h):
            src = products[(n, h)]
            dst = bank("ob%d" % h)
            for i in range(NT):
                col = slice(P * i, P * i + P)
                nc.tensor.matmul(out=dst[:, col], lhsT=src[:, col], rhs=ident_f[:], is_transpose=True, start=True, stop=False)
                nc.tensor.matmul(
                    out=dst[:, col], lhsT=src[:, BANK + P * i:BANK + P * i + P], rhs=swap_f[:],
                    is_transpose=True, start=False, stop=True,
                )
            back[(n, h)] = dst

        def store_head(n, h, copy):
            kind, a = UNITS[n]
            o = new_output()
            copy(out=o[:], in_=back[(n, h)][:])
            nc.sync.dma_start(
                out=outs[kind][2 * a + h, :, :].rearrange("(i p) f -> p i f", p=P),
                in_=o[:].rearrange("p (i f) -> p i f", i=NT),
            )

        def rotate_tokens(n, q):
            biased = new_biased()
            nc.vector.tensor_tensor(
                out=biased[:].rearrange("p (j f) -> p j f", j=2),
                in0=sums[(n, q)][:].rearrange("p (j f) -> p j f", j=2),
                in1=bias_q[:].rearrange("p (o f) -> p o f", o=1).to_broadcast([P, 2, UW]),
                op=ADD,
            )
            products[(n, q)] = new_products()
            for j in range(2):
                nc.vector.tensor_tensor(
                    out=products[(n, q)][:, BANK * j:BANK * j + BANK].rearrange("p (z h f) -> p z h f", z=2, h=2),
                    in0=biased[:, UW * j:UW * j + UW].rearrange("p (o h f) -> p o h f", o=1, h=2).to_broadcast([P, 2, 2, P]),
                    in1=cs[:, 2 * q + j, :, :].rearrange("p z (o f) -> p z o f", o=1).to_broadcast([P, 2, 2, P]),
                    op=MULT,
                )

        def store_tile(n, i, src):
            kind, a = UNITS[n]
            nc.sync.dma_start(
                out=outs[kind][2 * a:2 * a + 2, P * i:P * i + P, :].rearrange("h p f -> p h f"),
                in_=src.rearrange("p (h f) -> p h f", h=2),
            )

        def add_and_store_tokens(n, q):
            src = products[(n, q)][:].rearrange("p (j z h w f) -> p j z h w f", j=2, z=2, h=2, w=2)
            o = new_output()
            for j in range(2):
                nc.vector.tensor_tensor(
                    out=o[:, UW * j:UW * j + UW].rearrange("p (h w f) -> p h w f", h=2, w=2),
                    in0=src[:, j, 0, :, :, :],
                    in1=src[:, j, 1, :, ::-1, :],
                    op=ADD,
                )
            for j in range(2):
                store_tile(n, 2 * q + j, o[:, UW * j:UW * j + UW])

        def finish_v(n, q):
            a = UNITS[n][1]
            o = new_output()
            nc.vector.tensor_tensor(
                out=o[:].rearrange("p (j f) -> p j f", j=2),
                in0=sums[(n, q)][:].rearrange("p (j f) -> p j f", j=2),
                in1=bias_v[:, UW * a:UW * a + UW].rearrange("p (o f) -> p o f", o=1).to_broadcast([P, 2, UW]),
                op=ADD,
            )
            for j in range(2):
                store_tile(n, 2 * q + j, o[:, UW * j:UW * j + UW])

        def finish_last_v(q):
            a = UNITS[LAST_V][1]
            o = new_output()
            for j in range(2):
                part = o[:, UW * j:UW * j + UW]
                nc.vector.tensor_tensor(out=part, in0=sums[(LAST_V, q, j)], in1=bias_v[:, UW * a:UW * a + UW], op=ADD)
                store_tile(LAST_V, 2 * q + j, part)

        wide_first = work.tile([P, NG, 2, 512], BF16, name="wide_first", tag="wide_first", bufs=1)
        for g in range(NG):
            for t in range(2):
                widen = nc.vector.tensor_copy if (g, t) == (0, 1) else nc.scalar.copy
                widen(out=wide_first[:, g, t, :], in_=wq_first[g][:, t, :].bitcast(FP8))
        for g in range(NG):
            turned[(FIRST_Q, g)] = bank("tp%d" % g)
            tiles = []
            for t in range(2):
                w = wide_first[:, g, t, :].bitcast(F32)
                tiles.append((w[:, 0:256:2], w[:, 1:256:2], False))
            transpose_pass(turned[(FIRST_Q, g)], tiles)

        x_groups = [new_group(), new_group()]
        for q in range(2):
            for g in range(NG):
                dst = bank(("ac0", "ac1", "ob0", "ob1")[g])
                tiles = []
                for t in range(2):
                    w = x_sb[2 * q + t][:].bitcast(F32)
                    tiles.append((words_of_pass(w, False, g, 0), words_of_pass(w, False, g, 1), False))
                transpose_pass(dst, tiles)
                empty_bank(nc.scalar.copy, dst, True, x_groups[g // 2], 2048 * (g % 2) + 1024 * q)
        bias_cols = const.tile([P, 24], F32, name="bias_cols")
        tables = const.tile([P, 2 * BANK], BF16, name="tables")

        x_codes = []
        x_planes = []

        def quantize_x():
            for j in range(2):
                x_codes.append(const.tile([P, 1024], U32, name="x_codes%d" % j, align_bytes=64))
                x_planes.append(const.tile([P, 1024], U8, name="x_planes%d" % j, align_bytes=64))
            for q in range(2):
                for g in range(NG):
                    col = 512 * (g % 2) + 256 * q
                    nc.vector.quantize_mx(
                        out=x_codes[g // 2][:, col:col + 256].bitcast(FP8X4),
                        scales=x_planes[g // 2][:, col:col + 256],
                        in_=x_groups[g // 2][:, 4 * col:4 * col + 1024],
                    )

        def make_tables():
            dst = psum.tile([P, P], BF16, name="ob0", tag="ob0")
            nc.tensor.transpose(dst[:], bias_rows[:], ident_b[:])
            nc.scalar.copy(out=bias_cols[:], in_=dst[:, 0:24])
            dst = psum.tile([P, 2 * BANK], BF16, name="ob1", tag="ob1")
            for z in range(2):
                for i in range(NT):
                    col = BANK * z + P * i
                    nc.tensor.transpose(dst[:, col:col + P], cs[:, i, z, :], ident_b[:])
            nc.scalar.copy(out=tables[:], in_=dst[:])

        for s in range(-1, LAST_Q):
            for half in range(2):
                if s >= 0:
                    multiply_head(s, half)
                    if s == 0 and half == 0:
                        make_tables()
                    if (s, half) != (LAST_Q - 1, 1):
                        rotate_head(s, half)
                prepare(s + 3, half)
                for g in (2 * half, 2 * half + 1):
                    if UNITS[s + 1][0] == "q" or s + 1 == FIRST_K:
                        fill(s + 1, g)
                    if s + 2 == FIRST_K:
                        if g == NG - 1:
                            turn_first_k()
                    else:
                        turn(s + 2, g)
                if s >= 1:
                    turn_back(s - 1, half)
                    if half == 0:
                        store_head(s - 1, 0, nc.scalar.copy)
            quantize(s + 1)
            if s == -1:
                quantize_x()
            if s == LAST_Q - 1:
                rotate_head_on_vector(s, 1)
            if s >= 1:
                store_head(s - 1, 1, nc.scalar.copy)

        for half in range(2):
            multiply_tokens(LAST_Q, half, ("ac%d" % half,))
            rotate_tokens(LAST_Q, half)
            if half == 0:
                quantize(LAST_K)
            prepare(LAST_V, half)
            for g in (2 * half, 2 * half + 1):
                turn(FIRST_V, g)
            turn_back(LAST_Q - 1, half)
            if half == 0:
                store_head(LAST_Q - 1, 0, nc.vector.tensor_copy)
        store_head(LAST_Q - 1, 1, nc.scalar.copy)

        quantize(FIRST_V)
        for half in range(2):
            multiply_head(LAST_K, half)
            for g in (2 * half, 2 * half + 1):
                turn(LAST_V, g)
            rotate_head_on_vector(LAST_K, half)
        for q in range(2):
            add_and_store_tokens(LAST_Q, q)

        for half in range(2):
            multiply_tokens(FIRST_V, half, ("ac%d" % half,))
            turn_back(LAST_K, half)
            if half == 0:
                store_head(LAST_K, 0, nc.scalar.copy)
        quantize(LAST_V)
        for q in range(2):
            finish_v(FIRST_V, q)
        store_head(LAST_K, 1, nc.scalar.copy)

        for q in range(2):
            multiply_tokens(LAST_V, q, ("tp%d" % (2 * q), "tp%d" % (2 * q + 1)))
        for q in range(2):
            finish_last_v(q)
